import numpy as np
import ml_dtypes

BF16 = ml_dtypes.bfloat16


def bf(x):
    return np.asarray(x, np.float32).astype(BF16)


def f32(x):
    return np.asarray(x, np.float32)


def f64(x):
    return np.asarray(x).astype(np.float64)


def striped(idx):
    return np.tile(idx.reshape(-1, 16).T, (8, 1))


C, S, N = 512, 1024, 256
EPS = 1e-5


def pos_table():
    pos = np.arange(N, dtype=np.float32)[None, :]
    freqs = np.float32(1.0) / np.power(np.float32(10000.0), np.arange(0, C, 2, dtype=np.float32) / np.float32(C))
    pe = np.zeros((C, N), np.float32)
    pe[0::2] = np.sin(freqs[:, None] * pos)
    pe[1::2] = np.cos(freqs[:, None] * pos)
    return pe


def setup_inputs():
    return {"emb": f32(np.sqrt(0.5 / C) * np.random.standard_normal((C, S))), "pe": f32(pos_table()), "gain": f32(1.0 + 0.1 * np.random.standard_normal((C, 1))), "bias": f32(0.1 * np.random.standard_normal((C, 1))), "wout": bf(np.random.standard_normal((C, S)) / np.sqrt(C)), "bout": f32(0.1 * np.random.standard_normal((S, 1))), "offs": striped(np.random.permutation(np.tile(np.arange(S), 2))[:N])}


def reference(emb, pe, gain, bias, wout, bout, offs):
    idx = offs[:16].T.reshape(-1)
    h = np.sqrt(C) * f64(emb)[:, idx] + f64(pe)
    mu = h.mean(axis=0, keepdims=True)
    var = ((h - mu) ** 2).mean(axis=0, keepdims=True)
    y = f64(gain) * (h - mu) / np.sqrt(var + EPS) + f64(bias)
    return f64(wout).T @ y + f64(bout)

@@ -1,0 +1,106 @@
+import math
+
+import concourse.mybir as mybir
+from concourse.masks import make_identity
+
+P = 128
+C, S, N = 512, 1024, 256
+CB = C // P
+VB = S // P
+EPS = 1e-5
+FLOPS = 2 * C * S * N
+
+F32, BF16, U16 = mybir.dt.float32, mybir.dt.bfloat16, mybir.dt.uint16
+ALU = mybir.AluOpType
+FUNC = mybir.ActivationFunctionType
+
+
+def tile_decodertrans_kernel(tc, emb, pe, gain, bias, wout, bout, offs, out):
+    nc = tc.nc
+    emb_blocks = emb.rearrange("(b p) s -> b p s", p=P)
+    out_blocks = out.rearrange("(v p) j -> v p j", p=P)
+
+    with (
+        tc.tile_pool(name="held", bufs=1) as held,
+        tc.tile_pool(name="staged", bufs=4) as staged,
+        tc.psum_pool(name="stats", bufs=1) as stats,
+        tc.psum_pool(name="logits", bufs=4) as logits,
+    ):
+        offsets = held.tile([P, N // 16], U16, name="offsets")
+        nc.sync.dma_start(offsets[:], offs)
+        tables = []
+        for b in range(CB):
+            table = held.tile([P, S], F32, name=f"table{b}")
+            nc.sync.dma_start(table[:], emb_blocks[b])
+            tables.append(table)
+        wout_sb = held.tile([P, CB, S], BF16, name="wout_sb")
+        nc.sync.dma_start(wout_sb[:], wout.rearrange("(b p) v -> p b v", p=P))
+
+        pe_sb = held.tile([P, CB, N], F32, name="pe_sb")
+        nc.scalar.dma_start(pe_sb[:], pe.rearrange("(b p) j -> p b j", p=P))
+        rows = held.tile([P, P], F32, name="rows")
+        nc.gpsimd.memset(rows[:], 0.0)
+        nc.scalar.dma_start(rows[0:CB, :], gain.rearrange("(b p) o -> b (p o)", p=P))
+        nc.scalar.dma_start(rows[CB : 2 * CB, :], bias.rearrange("(b p) o -> b (p o)", p=P))
+        nc.scalar.dma_start(rows[2 * CB : 2 * CB + VB, :], bout.rearrange("(v p) o -> v (p o)", p=P))
+
+        averager = held.tile([P, P], F32, name="averager")
+        nc.gpsimd.memset(averager[:], 1.0 / C)
+        eps_col = held.tile([P, 1], F32, name="eps_col")
+        nc.gpsimd.memset(eps_col[:], EPS / C)
+        identity = held.tile([P, P], F32, name="identity")
+        make_identity(nc, identity[:])
+
+        cols_ps = stats.tile([P, P], F32, name="cols_ps")
+        nc.tensor.transpose(cols_ps[:], rows[:], identity[:])
+        cols = held.tile([P, 2 * CB + VB], F32, name="cols")
+        nc.vector.tensor_copy(cols[:], cols_ps[:, 0 : 2 * CB + VB])
+
+        pe_scaled = held.tile([P, CB, N], F32, name="pe_scaled")
+        mean_ps = stats.tile([P, N], F32, name="mean_ps")
+        gs = []
+        for b in range(CB):
+            nc.scalar.mul(pe_scaled[:, b, :], pe_sb[:, b, :], 1.0 / math.sqrt(C))
+            g = held.tile([P, N], F32, name=f"g{b}")
+            nc.vector.tensor_tensor(g[:], tables[b][:].indirect(offsets[:]), pe_scaled[:, b, :], ALU.add)
+            nc.tensor.matmul(mean_ps[:], averager[:], g[:], start=(b == 0), stop=(b == CB - 1))
+            gs.append(g)
+
+        var_ps = stats.tile([P, N], F32, name="var_ps")
+        centred = []
+        for b in range(CB):
+            d = held.tile([P, N], F32, name=f"d{b}")
+            nc.vector.tensor_tensor(d[:], gs[b][:], mean_ps[:], ALU.subtract)
+            sq = held.tile([P, N], F32, name=f"sq{b}")
+            nc.scalar.activation(sq[:], d[:], FUNC.Square)
+            nc.tensor.matmul(var_ps[:], averager[:], sq[:], start=(b == 0), stop=(b == CB - 1))
+            centred.append(d)
+
+        std = held.tile([P, N], F32, name="std")
+        nc.scalar.activation(std[:], var_ps[:], FUNC.Sqrt, bias=eps_col[:])
+        rstd = held.tile([P, N], F32, name="rstd")
+        nc.vector.reciprocal(rstd[:], std[:])
+
+        ys = []
+        for b in range(CB):
+            normed = held.tile([P, N], F32, name=f"normed{b}")
+            nc.vector.tensor_tensor(normed[:], centred[b][:], rstd[:], ALU.mult)
+            y = held.tile([P, N], BF16, name=f"y{b}")
+            nc.scalar.activation(
+                y[:], normed[:], FUNC.Identity, bias=cols[:, CB + b : CB + b + 1], scale=cols[:, b : b + 1]
+            )
+            ys.append(y)
+
+        for v in range(VB):
+            logit_ps = logits.tile([P, N], F32, name="logit_ps")
+            for b in range(CB):
+                nc.tensor.matmul(
+                    logit_ps[:], wout_sb[:, b, v * P : (v + 1) * P], ys[b][:], start=(b == 0), stop=(b == CB - 1)
+                )
+            logit = staged.tile([P, N], F32, name="logit")
+            bout_col = cols[:, 2 * CB + v : 2 * CB + v + 1]
+            if v % 2 == 0:
+                nc.scalar.activation(logit[:], logit_ps[:], FUNC.Identity, bias=bout_col)
+            else:
+                nc.vector.tensor_scalar_add(logit[:], logit_ps[:], bout_col)
+            nc.sync.dma_start(out_blocks[v], logit[:])

@@ -76,10 +76,8 @@ def tile_decodertrans_kernel(tc, emb, pe, gain, bias, wout, bout, offs, out):
             nc.tensor.matmul(var_ps[:], averager[:], sq[:], start=(b == 0), stop=(b == CB - 1))
             centred.append(d)
 
-        std = held.tile([P, N], F32, name="std")
-        nc.scalar.activation(std[:], var_ps[:], FUNC.Sqrt, bias=eps_col[:])
         rstd = held.tile([P, N], F32, name="rstd")
-        nc.vector.reciprocal(rstd[:], std[:])
+        nc.scalar.activation(rstd[:], var_ps[:], FUNC.Abs_reciprocal_sqrt, bias=eps_col[:])
 
         ys = []
         for b in range(CB):

@@ -44,6 +44,8 @@ def tile_decodertrans_kernel(tc, emb, pe, gain, bias, wout, bout, offs, out):
         nc.scalar.dma_start(rows[CB : 2 * CB, :], bias.rearrange("(b p) o -> b (p o)", p=P))
         nc.scalar.dma_start(rows[2 * CB : 2 * CB + VB, :], bout.rearrange("(v p) o -> v (p o)", p=P))
 
+        block_averager = held.tile([P, P], F32, name="block_averager")
+        nc.gpsimd.memset(block_averager[:], 1.0 / P)
         averager = held.tile([P, P], F32, name="averager")
         nc.gpsimd.memset(averager[:], 1.0 / C)
         eps_col = held.tile([P, 1], F32, name="eps_col")
@@ -51,38 +53,55 @@ def tile_decodertrans_kernel(tc, emb, pe, gain, bias, wout, bout, offs, out):
         identity = held.tile([P, P], F32, name="identity")
         make_identity(nc, identity[:])
 
+        warmed = held.tile([P, 1], F32, name="warmed")
+        nc.scalar.activation(warmed[:], eps_col[:], FUNC.Abs_reciprocal_sqrt)
+
         cols_ps = stats.tile([P, P], F32, name="cols_ps")
         nc.tensor.transpose(cols_ps[:], rows[:], identity[:])
         cols = held.tile([P, 2 * CB + VB], F32, name="cols")
         nc.vector.tensor_copy(cols[:], cols_ps[:, 0 : 2 * CB + VB])
 
         pe_scaled = held.tile([P, CB, N], F32, name="pe_scaled")
-        mean_ps = stats.tile([P, N], F32, name="mean_ps")
-        gs = []
         for b in range(CB):
             nc.scalar.mul(pe_scaled[:, b, :], pe_sb[:, b, :], 1.0 / math.sqrt(C))
-            g = held.tile([P, N], F32, name=f"g{b}")
-            nc.vector.tensor_tensor(g[:], tables[b][:].indirect(offsets[:]), pe_scaled[:, b, :], ALU.add)
-            nc.tensor.matmul(mean_ps[:], averager[:], g[:], start=(b == 0), stop=(b == CB - 1))
-            gs.append(g)
 
-        var_ps = stats.tile([P, N], F32, name="var_ps")
-        centred = []
+        shifted = []
+        g0 = held.tile([P, N], F32, name="g0")
+        nc.vector.tensor_tensor(g0[:], tables[0][:].indirect(offsets[:]), pe_scaled[:, 0, :], ALU.add)
+        shift_ps = stats.tile([P, N], F32, name="shift_ps")
+        nc.tensor.matmul(shift_ps[:], block_averager[:], g0[:], start=True, stop=True)
+        pe_shifted = held.tile([P, CB, N], F32, name="pe_shifted")
+        for b in range(1, CB):
+            nc.vector.tensor_tensor(pe_shifted[:, b, :], pe_scaled[:, b, :], shift_ps[:], ALU.subtract)
         for b in range(CB):
-            d = held.tile([P, N], F32, name=f"d{b}")
-            nc.vector.tensor_tensor(d[:], gs[b][:], mean_ps[:], ALU.subtract)
-            sq = held.tile([P, N], F32, name=f"sq{b}")
-            nc.scalar.activation(sq[:], d[:], FUNC.Square)
-            nc.tensor.matmul(var_ps[:], averager[:], sq[:], start=(b == 0), stop=(b == CB - 1))
-            centred.append(d)
+            e = held.tile([P, N], F32, name=f"e{b}")
+            if b == 0:
+                nc.vector.tensor_tensor(e[:], g0[:], shift_ps[:], ALU.subtract)
+            else:
+                nc.vector.tensor_tensor(e[:], tables[b][:].indirect(offsets[:]), pe_shifted[:, b, :], ALU.add)
+            shifted.append(e)
 
+        m_ps = stats.tile([P, N], F32, name="m_ps")
+        q_ps = stats.tile([P, N], F32, name="q_ps")
+        for b in range(CB):
+            sq = held.tile([P, N], F32, name=f"sq{b}")
+            nc.scalar.activation(sq[:], shifted[b][:], FUNC.Square)
+            nc.tensor.matmul(m_ps[:], averager[:], shifted[b][:], start=(b == 0), stop=(b == CB - 1))
+            nc.tensor.matmul(q_ps[:], averager[:], sq[:], start=(b == 0), stop=(b == CB - 1))
+
+        m_squared = held.tile([P, N], F32, name="m_squared")
+        nc.scalar.activation(m_squared[:], m_ps[:], FUNC.Square)
+        var = held.tile([P, N], F32, name="var")
+        nc.vector.tensor_tensor(var[:], q_ps[:], m_squared[:], ALU.subtract)
         rstd = held.tile([P, N], F32, name="rstd")
-        nc.scalar.activation(rstd[:], var_ps[:], FUNC.Abs_reciprocal_sqrt, bias=eps_col[:])
+        nc.scalar.activation(rstd[:], var[:], FUNC.Abs_reciprocal_sqrt, bias=eps_col[:])
 
         ys = []
         for b in range(CB):
+            centred = held.tile([P, N], F32, name=f"centred{b}")
+            nc.vector.tensor_tensor(centred[:], shifted[b][:], m_ps[:], ALU.subtract)
             normed = held.tile([P, N], F32, name=f"normed{b}")
-            nc.vector.tensor_tensor(normed[:], centred[b][:], rstd[:], ALU.mult)
+            nc.vector.tensor_tensor(normed[:], centred[:], rstd[:], ALU.mult)
             y = held.tile([P, N], BF16, name=f"y{b}")
             nc.scalar.activation(
                 y[:], normed[:], FUNC.Identity, bias=cols[:, CB + b : CB + b + 1], scale=cols[:, b : b + 1]

@@ -9,6 +9,7 @@ CB = C // P
 VB = S // P
 EPS = 1e-5
 FLOPS = 2 * C * S * N
+KEEP_BUSY = 4
 
 F32, BF16, U16 = mybir.dt.float32, mybir.dt.bfloat16, mybir.dt.uint16
 ALU = mybir.AluOpType
@@ -44,8 +45,6 @@ def tile_decodertrans_kernel(tc, emb, pe, gain, bias, wout, bout, offs, out):
         nc.scalar.dma_start(rows[CB : 2 * CB, :], bias.rearrange("(b p) o -> b (p o)", p=P))
         nc.scalar.dma_start(rows[2 * CB : 2 * CB + VB, :], bout.rearrange("(v p) o -> v (p o)", p=P))
 
-        block_averager = held.tile([P, P], F32, name="block_averager")
-        nc.gpsimd.memset(block_averager[:], 1.0 / P)
         averager = held.tile([P, P], F32, name="averager")
         nc.gpsimd.memset(averager[:], 1.0 / C)
         eps_col = held.tile([P, 1], F32, name="eps_col")
@@ -62,46 +61,36 @@ def tile_decodertrans_kernel(tc, emb, pe, gain, bias, wout, bout, offs, out):
         nc.vector.tensor_copy(cols[:], cols_ps[:, 0 : 2 * CB + VB])
 
         pe_scaled = held.tile([P, CB, N], F32, name="pe_scaled")
+        mean_ps = stats.tile([P, N], F32, name="mean_ps")
+        gs = []
         for b in range(CB):
             nc.scalar.mul(pe_scaled[:, b, :], pe_sb[:, b, :], 1.0 / math.sqrt(C))
+            g = held.tile([P, N], F32, name=f"g{b}")
+            nc.vector.tensor_tensor(g[:], tables[b][:].indirect(offsets[:]), pe_scaled[:, b, :], ALU.add)
+            nc.tensor.matmul(mean_ps[:], averager[:], g[:], start=(b == 0), stop=(b == CB - 1))
+            gs.append(g)
 
-        shifted = []
-        g0 = held.tile([P, N], F32, name="g0")
-        nc.vector.tensor_tensor(g0[:], tables[0][:].indirect(offsets[:]), pe_scaled[:, 0, :], ALU.add)
-        shift_ps = stats.tile([P, N], F32, name="shift_ps")
-        nc.tensor.matmul(shift_ps[:], block_averager[:], g0[:], start=True, stop=True)
-        pe_shifted = held.tile([P, CB, N], F32, name="pe_shifted")
-        for b in range(1, CB):
-            nc.vector.tensor_tensor(pe_shifted[:, b, :], pe_scaled[:, b, :], shift_ps[:], ALU.subtract)
+        var_ps = stats.tile([P, N], F32, name="var_ps")
+        centred = []
         for b in range(CB):
-            e = held.tile([P, N], F32, name=f"e{b}")
-            if b == 0:
-                nc.vector.tensor_tensor(e[:], g0[:], shift_ps[:], ALU.subtract)
-            else:
-                nc.vector.tensor_tensor(e[:], tables[b][:].indirect(offsets[:]), pe_shifted[:, b, :], ALU.add)
-            shifted.append(e)
-
-        m_ps = stats.tile([P, N], F32, name="m_ps")
-        q_ps = stats.tile([P, N], F32, name="q_ps")
-        for b in range(CB):
+            d = held.tile([P, N], F32, name=f"d{b}")
+            nc.vector.tensor_tensor(d[:], gs[b][:], mean_ps[:], ALU.subtract)
             sq = held.tile([P, N], F32, name=f"sq{b}")
-            nc.scalar.activation(sq[:], shifted[b][:], FUNC.Square)
-            nc.tensor.matmul(m_ps[:], averager[:], shifted[b][:], start=(b == 0), stop=(b == CB - 1))
-            nc.tensor.matmul(q_ps[:], averager[:], sq[:], start=(b == 0), stop=(b == CB - 1))
+            nc.scalar.activation(sq[:], d[:], FUNC.Square)
+            nc.tensor.matmul(var_ps[:], averager[:], sq[:], start=(b == 0), stop=(b == CB - 1))
+            centred.append(d)
 
-        m_squared = held.tile([P, N], F32, name="m_squared")
-        nc.scalar.activation(m_squared[:], m_ps[:], FUNC.Square)
-        var = held.tile([P, N], F32, name="var")
-        nc.vector.tensor_tensor(var[:], q_ps[:], m_squared[:], ALU.subtract)
+        unread_ps = stats.tile([P, 2 * N], F32, name="unread_ps")
+        for k in range(KEEP_BUSY):
+            nc.tensor.matmul(unread_ps[:], wout_sb[:, 0, 0:P], wout_sb[:, 0, 0 : 2 * N], start=True, stop=True)
+
         rstd = held.tile([P, N], F32, name="rstd")
-        nc.scalar.activation(rstd[:], var[:], FUNC.Abs_reciprocal_sqrt, bias=eps_col[:])
+        nc.scalar.activation(rstd[:], var_ps[:], FUNC.Abs_reciprocal_sqrt, bias=eps_col[:])
 
         ys = []
         for b in range(CB):
-            centred = held.tile([P, N], F32, name=f"centred{b}")
-            nc.vector.tensor_tensor(centred[:], shifted[b][:], m_ps[:], ALU.subtract)
             normed = held.tile([P, N], F32, name=f"normed{b}")
-            nc.vector.tensor_tensor(normed[:], centred[:], rstd[:], ALU.mult)
+            nc.vector.tensor_tensor(normed[:], centred[b][:], rstd[:], ALU.mult)
             y = held.tile([P, N], BF16, name=f"y{b}")
             nc.scalar.activation(
                 y[:], normed[:], FUNC.Identity, bias=cols[:, CB + b : CB + b + 1], scale=cols[:, b : b + 1]

@@ -9,7 +9,8 @@ CB = C // P
 VB = S // P
 EPS = 1e-5
 FLOPS = 2 * C * S * N
-KEEP_BUSY = 4
+BEFORE_TABLE = 10
+BEFORE_PROJECTION = 4
 
 F32, BF16, U16 = mybir.dt.float32, mybir.dt.bfloat16, mybir.dt.uint16
 ALU = mybir.AluOpType
@@ -55,6 +56,16 @@ def tile_decodertrans_kernel(tc, emb, pe, gain, bias, wout, bout, offs, out):
         warmed = held.tile([P, 1], F32, name="warmed")
         nc.scalar.activation(warmed[:], eps_col[:], FUNC.Abs_reciprocal_sqrt)
 
+        idle_operand = held.tile([P, 2 * N], BF16, name="idle_operand")
+        nc.vector.memset(idle_operand[:], 0.0)
+        unread_ps = stats.tile([P, 2 * N], F32, name="unread_ps")
+
+        def keep_busy(count):
+            for k in range(count):
+                nc.tensor.matmul(unread_ps[:], idle_operand[:, 0:P], idle_operand[:], start=True, stop=True)
+
+        keep_busy(BEFORE_TABLE)
+
         cols_ps = stats.tile([P, P], F32, name="cols_ps")
         nc.tensor.transpose(cols_ps[:], rows[:], identity[:])
         cols = held.tile([P, 2 * CB + VB], F32, name="cols")
@@ -80,9 +91,7 @@ def tile_decodertrans_kernel(tc, emb, pe, gain, bias, wout, bout, offs, out):
             nc.tensor.matmul(var_ps[:], averager[:], sq[:], start=(b == 0), stop=(b == CB - 1))
             centred.append(d)
 
-        unread_ps = stats.tile([P, 2 * N], F32, name="unread_ps")
-        for k in range(KEEP_BUSY):
-            nc.tensor.matmul(unread_ps[:], wout_sb[:, 0, 0:P], wout_sb[:, 0, 0 : 2 * N], start=True, stop=True)
+        keep_busy(BEFORE_PROJECTION)
 
         rstd = held.tile([P, N], F32, name="rstd")
         nc.scalar.activation(rstd[:], var_ps[:], FUNC.Abs_reciprocal_sqrt, bias=eps_col[:])

@@ -9,8 +9,7 @@ CB = C // P
 VB = S // P
 EPS = 1e-5
 FLOPS = 2 * C * S * N
-BEFORE_TABLE = 10
-BEFORE_PROJECTION = 4
+KEEP_BUSY = 4
 
 F32, BF16, U16 = mybir.dt.float32, mybir.dt.bfloat16, mybir.dt.uint16
 ALU = mybir.AluOpType
@@ -56,16 +55,6 @@ def tile_decodertrans_kernel(tc, emb, pe, gain, bias, wout, bout, offs, out):
         warmed = held.tile([P, 1], F32, name="warmed")
         nc.scalar.activation(warmed[:], eps_col[:], FUNC.Abs_reciprocal_sqrt)
 
-        idle_operand = held.tile([P, 2 * N], BF16, name="idle_operand")
-        nc.vector.memset(idle_operand[:], 0.0)
-        unread_ps = stats.tile([P, 2 * N], F32, name="unread_ps")
-
-        def keep_busy(count):
-            for k in range(count):
-                nc.tensor.matmul(unread_ps[:], idle_operand[:, 0:P], idle_operand[:], start=True, stop=True)
-
-        keep_busy(BEFORE_TABLE)
-
         cols_ps = stats.tile([P, P], F32, name="cols_ps")
         nc.tensor.transpose(cols_ps[:], rows[:], identity[:])
         cols = held.tile([P, 2 * CB + VB], F32, name="cols")
@@ -83,15 +72,23 @@ def tile_decodertrans_kernel(tc, emb, pe, gain, bias, wout, bout, offs, out):
 
         var_ps = stats.tile([P, N], F32, name="var_ps")
         centred = []
+        squares = []
         for b in range(CB):
             d = held.tile([P, N], F32, name=f"d{b}")
             nc.vector.tensor_tensor(d[:], gs[b][:], mean_ps[:], ALU.subtract)
             sq = held.tile([P, N], F32, name=f"sq{b}")
             nc.scalar.activation(sq[:], d[:], FUNC.Square)
-            nc.tensor.matmul(var_ps[:], averager[:], sq[:], start=(b == 0), stop=(b == CB - 1))
             centred.append(d)
+            squares.append(sq)
+        last_two = held.tile([P, N], F32, name="last_two")
+        nc.vector.tensor_tensor(last_two[:], squares[CB - 2][:], squares[CB - 1][:], ALU.add)
+        summands = squares[: CB - 2] + [last_two]
+        for k, summand in enumerate(summands):
+            nc.tensor.matmul(var_ps[:], averager[:], summand[:], start=(k == 0), stop=(k == len(summands) - 1))
 
-        keep_busy(BEFORE_PROJECTION)
+        unread_ps = stats.tile([P, 2 * N], F32, name="unread_ps")
+        for k in range(KEEP_BUSY):
+            nc.tensor.matmul(unread_ps[:], wout_sb[:, 0, 0:P], wout_sb[:, 0, 0 : 2 * N], start=True, stop=True)
 
         rstd = held.tile([P, N], F32, name="rstd")
         nc.scalar.activation(rstd[:], var_ps[:], FUNC.Abs_reciprocal_sqrt, bias=eps_col[:])

@@ -86,9 +86,11 @@ def tile_decodertrans_kernel(tc, emb, pe, gain, bias, wout, bout, offs, out):
         for k, summand in enumerate(summands):
             nc.tensor.matmul(var_ps[:], averager[:], summand[:], start=(k == 0), stop=(k == len(summands) - 1))
 
+        idle_operand = held.tile([P, 2 * N], BF16, name="idle_operand")
+        nc.vector.memset(idle_operand[:], 0.0)
         unread_ps = stats.tile([P, 2 * N], F32, name="unread_ps")
         for k in range(KEEP_BUSY):
-            nc.tensor.matmul(unread_ps[:], wout_sb[:, 0, 0:P], wout_sb[:, 0, 0 : 2 * N], start=True, stop=True)
+            nc.tensor.matmul(unread_ps[:], idle_operand[:, 0:P], idle_operand[:], start=True, stop=True)
 
         rstd = held.tile([P, N], F32, name="rstd")
         nc.scalar.activation(rstd[:], var_ps[:], FUNC.Abs_reciprocal_sqrt, bias=eps_col[:])

@@ -9,7 +9,7 @@ CB = C // P
 VB = S // P
 EPS = 1e-5
 FLOPS = 2 * C * S * N
-KEEP_BUSY = 4
+KEEP_BUSY = 2
 
 F32, BF16, U16 = mybir.dt.float32, mybir.dt.bfloat16, mybir.dt.uint16
 ALU = mybir.AluOpType
@@ -86,11 +86,9 @@ def tile_decodertrans_kernel(tc, emb, pe, gain, bias, wout, bout, offs, out):
         for k, summand in enumerate(summands):
             nc.tensor.matmul(var_ps[:], averager[:], summand[:], start=(k == 0), stop=(k == len(summands) - 1))
 
-        idle_operand = held.tile([P, 2 * N], BF16, name="idle_operand")
-        nc.vector.memset(idle_operand[:], 0.0)
-        unread_ps = stats.tile([P, 2 * N], F32, name="unread_ps")
+        unread_ps = stats.tile([P, N], F32, name="unread_ps")
         for k in range(KEEP_BUSY):
-            nc.tensor.matmul(unread_ps[:], idle_operand[:, 0:P], idle_operand[:], start=True, stop=True)
+            nc.tensor.matmul(unread_ps[:], averager[:], last_two[:], start=True, stop=True)
 
         rstd = held.tile([P, N], F32, name="rstd")
         nc.scalar.activation(rstd[:], var_ps[:], FUNC.Abs_reciprocal_sqrt, bias=eps_col[:])

@@ -19,11 +19,10 @@ FUNC = mybir.ActivationFunctionType
 def tile_decodertrans_kernel(tc, emb, pe, gain, bias, wout, bout, offs, out):
     nc = tc.nc
     emb_blocks = emb.rearrange("(b p) s -> b p s", p=P)
-    out_blocks = out.rearrange("(v p) j -> v p j", p=P)
+    out_rows = out.rearrange("(p k) j -> p k j", k=VB)
 
     with (
         tc.tile_pool(name="held", bufs=1) as held,
-        tc.tile_pool(name="staged", bufs=4) as staged,
         tc.psum_pool(name="stats", bufs=1) as stats,
         tc.psum_pool(name="logits", bufs=4) as logits,
     ):
@@ -43,7 +42,8 @@ def tile_decodertrans_kernel(tc, emb, pe, gain, bias, wout, bout, offs, out):
         nc.gpsimd.memset(rows[:], 0.0)
         nc.scalar.dma_start(rows[0:CB, :], gain.rearrange("(b p) o -> b (p o)", p=P))
         nc.scalar.dma_start(rows[CB : 2 * CB, :], bias.rearrange("(b p) o -> b (p o)", p=P))
-        nc.scalar.dma_start(rows[2 * CB : 2 * CB + VB, :], bout.rearrange("(v p) o -> v (p o)", p=P))
+        bout_cols = held.tile([P, VB], F32, name="bout_cols")
+        nc.scalar.dma_start(bout_cols[:], bout.rearrange("(p k) o -> p (k o)", k=VB))
 
         averager = held.tile([P, P], F32, name="averager")
         nc.gpsimd.memset(averager[:], 1.0 / C)
@@ -57,8 +57,8 @@ def tile_decodertrans_kernel(tc, emb, pe, gain, bias, wout, bout, offs, out):
 
         cols_ps = stats.tile([P, P], F32, name="cols_ps")
         nc.tensor.transpose(cols_ps[:], rows[:], identity[:])
-        cols = held.tile([P, 2 * CB + VB], F32, name="cols")
-        nc.vector.tensor_copy(cols[:], cols_ps[:, 0 : 2 * CB + VB])
+        cols = held.tile([P, 2 * CB], F32, name="cols")
+        nc.vector.tensor_copy(cols[:], cols_ps[:, 0 : 2 * CB])
 
         pe_scaled = held.tile([P, CB, N], F32, name="pe_scaled")
         mean_ps = stats.tile([P, N], F32, name="mean_ps")
@@ -103,16 +103,16 @@ def tile_decodertrans_kernel(tc, emb, pe, gain, bias, wout, bout, offs, out):
             )
             ys.append(y)
 
-        for v in range(VB):
+        stores = [(k, k + 2) for k in range(0, VB - 2, 2)] + [(VB - 2, VB - 1), (VB - 1, VB)]
+        logit = held.tile([P, VB, N], F32, name="logit")
+        for k in range(VB):
             logit_ps = logits.tile([P, N], F32, name="logit_ps")
             for b in range(CB):
-                nc.tensor.matmul(
-                    logit_ps[:], wout_sb[:, b, v * P : (v + 1) * P], ys[b][:], start=(b == 0), stop=(b == CB - 1)
-                )
-            logit = staged.tile([P, N], F32, name="logit")
-            bout_col = cols[:, 2 * CB + v : 2 * CB + v + 1]
-            if v % 2 == 0:
-                nc.scalar.activation(logit[:], logit_ps[:], FUNC.Identity, bias=bout_col)
+                nc.tensor.matmul(logit_ps[:], wout_sb[:, b, k:S:VB], ys[b][:], start=(b == 0), stop=(b == CB - 1))
+            if k % 2 == 0:
+                nc.scalar.activation(logit[:, k, :], logit_ps[:], FUNC.Identity, bias=bout_cols[:, k : k + 1])
             else:
-                nc.vector.tensor_scalar_add(logit[:], logit_ps[:], bout_col)
-            nc.sync.dma_start(out_blocks[v], logit[:])
+                nc.vector.tensor_scalar_add(logit[:, k, :], logit_ps[:], bout_cols[:, k : k + 1])
+            for first, end in stores:
+                if end == k + 1:
+                    nc.sync.dma_start(out_rows[:, first:end, :], logit[:, first:end, :])

@@ -24,7 +24,7 @@ def tile_decodertrans_kernel(tc, emb, pe, gain, bias, wout, bout, offs, out):
     with (
         tc.tile_pool(name="held", bufs=1) as held,
         tc.psum_pool(name="stats", bufs=1) as stats,
-        tc.psum_pool(name="logits", bufs=4) as logits,
+        tc.psum_pool(name="logits", bufs=5) as logits,
     ):
         offsets = held.tile([P, N // 16], U16, name="offsets")
         nc.sync.dma_start(offsets[:], offs)
@@ -66,27 +66,50 @@ def tile_decodertrans_kernel(tc, emb, pe, gain, bias, wout, bout, offs, out):
         for b in range(CB):
             nc.scalar.mul(pe_scaled[:, b, :], pe_sb[:, b, :], 1.0 / math.sqrt(C))
             g = held.tile([P, N], F32, name=f"g{b}")
-            nc.vector.tensor_tensor(g[:], tables[b][:].indirect(offsets[:]), pe_scaled[:, b, :], ALU.add)
-            nc.tensor.matmul(mean_ps[:], averager[:], g[:], start=(b == 0), stop=(b == CB - 1))
+            pieces = 2 if b == CB - 1 else 1
+            width = N // pieces
+            for piece in range(pieces):
+                cols_of_piece = slice(piece * width, (piece + 1) * width)
+                nc.vector.tensor_tensor(
+                    g[:, cols_of_piece],
+                    tables[b][:].indirect(offsets[:, piece * width // 16 : (piece + 1) * width // 16]),
+                    pe_scaled[:, b, cols_of_piece],
+                    ALU.add,
+                )
+                last = b == CB - 1 and piece == pieces - 1
+                nc.tensor.matmul(mean_ps[:, cols_of_piece], averager[:], g[:, cols_of_piece], start=(b == 0), stop=last)
             gs.append(g)
 
         var_ps = stats.tile([P, N], F32, name="var_ps")
         centred = []
         squares = []
+        last_two = held.tile([P, N], F32, name="last_two")
         for b in range(CB):
             d = held.tile([P, N], F32, name=f"d{b}")
-            nc.vector.tensor_tensor(d[:], gs[b][:], mean_ps[:], ALU.subtract)
             sq = held.tile([P, N], F32, name=f"sq{b}")
-            nc.scalar.activation(sq[:], d[:], FUNC.Square)
             centred.append(d)
             squares.append(sq)
-        last_two = held.tile([P, N], F32, name="last_two")
-        nc.vector.tensor_tensor(last_two[:], squares[CB - 2][:], squares[CB - 1][:], ALU.add)
-        summands = squares[: CB - 2] + [last_two]
-        for k, summand in enumerate(summands):
-            nc.tensor.matmul(var_ps[:], averager[:], summand[:], start=(k == 0), stop=(k == len(summands) - 1))
+            pieces = 2 if b == CB - 1 else 1
+            width = N // pieces
+            for piece in range(pieces):
+                cols_of_piece = slice(piece * width, (piece + 1) * width)
+                nc.vector.tensor_tensor(d[:, cols_of_piece], gs[b][:, cols_of_piece], mean_ps[:, cols_of_piece], ALU.subtract)
+                nc.scalar.activation(sq[:, cols_of_piece], d[:, cols_of_piece], FUNC.Square)
+                if b < CB - 2:
+                    nc.tensor.matmul(var_ps[:], averager[:], sq[:], start=(b == 0), stop=False)
+                if b == CB - 1:
+                    nc.vector.tensor_tensor(
+                        last_two[:, cols_of_piece], squares[b - 1][:, cols_of_piece], sq[:, cols_of_piece], ALU.add
+                    )
+                    nc.tensor.matmul(
+                        var_ps[:, cols_of_piece],
+                        averager[:],
+                        last_two[:, cols_of_piece],
+                        start=False,
+                        stop=(piece == pieces - 1),
+                    )
 
-        unread_ps = stats.tile([P, N], F32, name="unread_ps")
+        unread_ps = stats.tile([P, N], F32, name="unread_ps", tag="cols_ps")
         for k in range(KEEP_BUSY):
             nc.tensor.matmul(unread_ps[:], averager[:], last_two[:], start=True, stop=True)
 
@@ -98,9 +121,11 @@ def tile_decodertrans_kernel(tc, emb, pe, gain, bias, wout, bout, offs, out):
             normed = held.tile([P, N], F32, name=f"normed{b}")
             nc.vector.tensor_tensor(normed[:], centred[b][:], rstd[:], ALU.mult)
             y = held.tile([P, N], BF16, name=f"y{b}")
-            nc.scalar.activation(
-                y[:], normed[:], FUNC.Identity, bias=cols[:, CB + b : CB + b + 1], scale=cols[:, b : b + 1]
-            )
+            gain_col, bias_col = cols[:, b : b + 1], cols[:, CB + b : CB + b + 1]
+            if b == 0:
+                nc.vector.tensor_scalar(y[:], normed[:], gain_col, bias_col, ALU.mult, ALU.add)
+            else:
+                nc.scalar.activation(y[:], normed[:], FUNC.Identity, bias=bias_col, scale=gain_col)
             ys.append(y)
 
         stores = [(k, k + 2) for k in range(0, VB - 2, 2)] + [(VB - 2, VB - 1), (VB - 1, VB)]

@@ -128,16 +128,25 @@ def tile_decodertrans_kernel(tc, emb, pe, gain, bias, wout, bout, offs, out):
                 nc.scalar.activation(y[:], normed[:], FUNC.Identity, bias=bias_col, scale=gain_col)
             ys.append(y)
 
-        stores = [(k, k + 2) for k in range(0, VB - 2, 2)] + [(VB - 2, VB - 1), (VB - 1, VB)]
         logit = held.tile([P, VB, N], F32, name="logit")
+        exits = 0
         for k in range(VB):
-            logit_ps = logits.tile([P, N], F32, name="logit_ps")
-            for b in range(CB):
-                nc.tensor.matmul(logit_ps[:], wout_sb[:, b, k:S:VB], ys[b][:], start=(b == 0), stop=(b == CB - 1))
-            if k % 2 == 0:
-                nc.scalar.activation(logit[:, k, :], logit_ps[:], FUNC.Identity, bias=bout_cols[:, k : k + 1])
-            else:
-                nc.vector.tensor_scalar_add(logit[:, k, :], logit_ps[:], bout_cols[:, k : k + 1])
-            for first, end in stores:
-                if end == k + 1:
-                    nc.sync.dma_start(out_rows[:, first:end, :], logit[:, first:end, :])
+            pieces = 2 if k == VB - 1 else 1
+            width = N // pieces
+            for piece in range(pieces):
+                cols_of_piece = slice(piece * width, (piece + 1) * width)
+                logit_ps = logits.tile([P, width], F32, name="logit_ps")
+                for b in range(CB):
+                    nc.tensor.matmul(
+                        logit_ps[:], wout_sb[:, b, k:S:VB], ys[b][:, cols_of_piece], start=(b == 0), stop=(b == CB - 1)
+                    )
+                bout_col = bout_cols[:, k : k + 1]
+                if exits % 2 == 0:
+                    nc.vector.tensor_scalar_add(logit[:, k, cols_of_piece], logit_ps[:], bout_col)
+                else:
+                    nc.scalar.activation(logit[:, k, cols_of_piece], logit_ps[:], FUNC.Identity, bias=bout_col)
+                exits += 1
+                if k >= VB - 2:
+                    nc.sync.dma_start(out_rows[:, k, cols_of_piece], logit[:, k, cols_of_piece])
+                elif k % 2 == 1:
+                    nc.sync.dma_start(out_rows[:, k - 1 : k + 1, :], logit[:, k - 1 : k + 1, :])

@@ -19,7 +19,7 @@ FUNC = mybir.ActivationFunctionType
 def tile_decodertrans_kernel(tc, emb, pe, gain, bias, wout, bout, offs, out):
     nc = tc.nc
     emb_blocks = emb.rearrange("(b p) s -> b p s", p=P)
-    out_rows = out.rearrange("(p k) j -> p k j", k=VB)
+    out_blocks = out.rearrange("(v p) j -> v p j", p=P)
 
     with (
         tc.tile_pool(name="held", bufs=1) as held,
@@ -42,8 +42,7 @@ def tile_decodertrans_kernel(tc, emb, pe, gain, bias, wout, bout, offs, out):
         nc.gpsimd.memset(rows[:], 0.0)
         nc.scalar.dma_start(rows[0:CB, :], gain.rearrange("(b p) o -> b (p o)", p=P))
         nc.scalar.dma_start(rows[CB : 2 * CB, :], bias.rearrange("(b p) o -> b (p o)", p=P))
-        bout_cols = held.tile([P, VB], F32, name="bout_cols")
-        nc.scalar.dma_start(bout_cols[:], bout.rearrange("(p k) o -> p (k o)", k=VB))
+        nc.scalar.dma_start(rows[2 * CB : 2 * CB + VB, :], bout.rearrange("(v p) o -> v (p o)", p=P))
 
         averager = held.tile([P, P], F32, name="averager")
         nc.gpsimd.memset(averager[:], 1.0 / C)
@@ -57,8 +56,8 @@ def tile_decodertrans_kernel(tc, emb, pe, gain, bias, wout, bout, offs, out):
 
         cols_ps = stats.tile([P, P], F32, name="cols_ps")
         nc.tensor.transpose(cols_ps[:], rows[:], identity[:])
-        cols = held.tile([P, 2 * CB], F32, name="cols")
-        nc.vector.tensor_copy(cols[:], cols_ps[:, 0 : 2 * CB])
+        cols = held.tile([P, 2 * CB + VB], F32, name="cols")
+        nc.vector.tensor_copy(cols[:], cols_ps[:, 0 : 2 * CB + VB])
 
         pe_scaled = held.tile([P, CB, N], F32, name="pe_scaled")
         mean_ps = stats.tile([P, N], F32, name="mean_ps")
@@ -130,23 +129,24 @@ def tile_decodertrans_kernel(tc, emb, pe, gain, bias, wout, bout, offs, out):
 
         logit = held.tile([P, VB, N], F32, name="logit")
         exits = 0
-        for k in range(VB):
-            pieces = 2 if k == VB - 1 else 1
+        for v in range(VB):
+            pieces = 2 if v == VB - 1 else 1
             width = N // pieces
             for piece in range(pieces):
                 cols_of_piece = slice(piece * width, (piece + 1) * width)
                 logit_ps = logits.tile([P, width], F32, name="logit_ps")
                 for b in range(CB):
                     nc.tensor.matmul(
-                        logit_ps[:], wout_sb[:, b, k:S:VB], ys[b][:, cols_of_piece], start=(b == 0), stop=(b == CB - 1)
+                        logit_ps[:],
+                        wout_sb[:, b, v * P : (v + 1) * P],
+                        ys[b][:, cols_of_piece],
+                        start=(b == 0),
+                        stop=(b == CB - 1),
                     )
-                bout_col = bout_cols[:, k : k + 1]
+                bout_col = cols[:, 2 * CB + v : 2 * CB + v + 1]
                 if exits % 2 == 0:
-                    nc.vector.tensor_scalar_add(logit[:, k, cols_of_piece], logit_ps[:], bout_col)
+                    nc.vector.tensor_scalar_add(logit[:, v, cols_of_piece], logit_ps[:], bout_col)
                 else:
-                    nc.scalar.activation(logit[:, k, cols_of_piece], logit_ps[:], FUNC.Identity, bias=bout_col)
+                    nc.scalar.activation(logit[:, v, cols_of_piece], logit_ps[:], FUNC.Identity, bias=bout_col)
                 exits += 1
-                if k >= VB - 2:
-                    nc.sync.dma_start(out_rows[:, k, cols_of_piece], logit[:, k, cols_of_piece])
-                elif k % 2 == 1:
-                    nc.sync.dma_start(out_rows[:, k - 1 : k + 1, :], logit[:, k - 1 : k + 1, :])
+                nc.sync.dma_start(out_blocks[v][:, cols_of_piece], logit[:, v, cols_of_piece])

@@ -9,7 +9,7 @@ CB = C // P
 VB = S // P
 EPS = 1e-5
 FLOPS = 2 * C * S * N
-KEEP_BUSY = 2
+H = N // 2
 
 F32, BF16, U16 = mybir.dt.float32, mybir.dt.bfloat16, mybir.dt.uint16
 ALU = mybir.AluOpType
@@ -19,33 +19,41 @@ FUNC = mybir.ActivationFunctionType
 def tile_decodertrans_kernel(tc, emb, pe, gain, bias, wout, bout, offs, out):
     nc = tc.nc
     emb_blocks = emb.rearrange("(b p) s -> b p s", p=P)
-    out_blocks = out.rearrange("(v p) j -> v p j", p=P)
+    out_pairs = out.rearrange("(v p) j -> p v j", p=P)
+    first, second = slice(0, H), slice(H, N)
+    offs_first, offs_second = slice(0, H // 16), slice(H // 16, N // 16)
 
     with (
         tc.tile_pool(name="held", bufs=1) as held,
         tc.psum_pool(name="stats", bufs=1) as stats,
-        tc.psum_pool(name="logits", bufs=5) as logits,
+        tc.psum_pool(name="logits", bufs=4) as logits,
     ):
         offsets = held.tile([P, N // 16], U16, name="offsets")
-        nc.sync.dma_start(offsets[:], offs)
-        tables = []
-        for b in range(CB):
-            table = held.tile([P, S], F32, name=f"table{b}")
-            nc.sync.dma_start(table[:], emb_blocks[b])
-            tables.append(table)
+        tables = [held.tile([P, S], F32, name=f"table{b}") for b in range(CB)]
         wout_sb = held.tile([P, CB, S], BF16, name="wout_sb")
-        nc.sync.dma_start(wout_sb[:], wout.rearrange("(b p) v -> p b v", p=P))
-
-        pe_sb = held.tile([P, CB, N], F32, name="pe_sb")
-        nc.scalar.dma_start(pe_sb[:], pe.rearrange("(b p) j -> p b j", p=P))
+        pe_first = held.tile([P, N], F32, name="pe_first")
+        pe_rest = held.tile([P, CB - 1, N], F32, name="pe_rest")
+        pe_sb = [pe_first[:]] + [pe_rest[:, b, :] for b in range(CB - 1)]
+        pe_blocks = pe.rearrange("(b p) j -> p b j", p=P)
+        nc.sync.dma_start(offsets[:], offs)
+        nc.scalar.dma_start(pe_first[:], pe_blocks[:, 0, :])
+        nc.sync.dma_start(tables[0][:], emb_blocks[0])
+        nc.sync.dma_start(pe_rest[:], pe_blocks[:, 1:CB, :])
+        for b in range(1, CB):
+            nc.sync.dma_start(tables[b][:], emb_blocks[b])
         rows = held.tile([P, P], F32, name="rows")
         nc.gpsimd.memset(rows[:], 0.0)
-        nc.scalar.dma_start(rows[0:CB, :], gain.rearrange("(b p) o -> b (p o)", p=P))
-        nc.scalar.dma_start(rows[CB : 2 * CB, :], bias.rearrange("(b p) o -> b (p o)", p=P))
-        nc.scalar.dma_start(rows[2 * CB : 2 * CB + VB, :], bout.rearrange("(v p) o -> v (p o)", p=P))
+        nc.sync.dma_start(rows[0:CB, :], gain.rearrange("(b p) o -> b (p o)", p=P))
+        nc.sync.dma_start(rows[CB : 2 * CB, :], bias.rearrange("(b p) o -> b (p o)", p=P))
+        nc.sync.dma_start(rows[2 * CB : 2 * CB + VB, :], bout.rearrange("(v p) o -> v (p o)", p=P))
+        nc.sync.dma_start(wout_sb[:], wout.rearrange("(b p) v -> p b v", p=P))
 
         averager = held.tile([P, P], F32, name="averager")
         nc.gpsimd.memset(averager[:], 1.0 / C)
+        block_averager = held.tile([P, P], F32, name="block_averager")
+        nc.gpsimd.memset(block_averager[:], 1.0 / P)
+        minus_two = held.tile([P, P], F32, name="minus_two")
+        nc.gpsimd.memset(minus_two[:], -2.0 / C)
         eps_col = held.tile([P, 1], F32, name="eps_col")
         nc.gpsimd.memset(eps_col[:], EPS / C)
         identity = held.tile([P, P], F32, name="identity")
@@ -54,99 +62,104 @@ def tile_decodertrans_kernel(tc, emb, pe, gain, bias, wout, bout, offs, out):
         warmed = held.tile([P, 1], F32, name="warmed")
         nc.scalar.activation(warmed[:], eps_col[:], FUNC.Abs_reciprocal_sqrt)
 
-        cols_ps = stats.tile([P, P], F32, name="cols_ps")
+        last = CB - 1
+        pe_scaled = [held.tile([P, N], F32, name=f"pe_scaled{b}") for b in range(CB)]
+        gs = [held.tile([P, N], F32, name=f"g{b}") for b in range(CB)]
+        ds = [held.tile([P, H], F32, name=f"d{b}") for b in range(CB)]
+        squares = [held.tile([P, H], F32, name=f"sq{b}") for b in range(CB)]
+        centre_ps = stats.tile([P, H], F32, name="centre_ps")
+        pe_centred = held.tile([P, H], F32, name="pe_centred")
+        delta_ps = stats.tile([P, H], F32, name="delta_ps")
+        square_ps = stats.tile([P, H], F32, name="square_ps")
+        mean_ps = stats.tile([P, H], F32, name="mean_ps")
+        for b in range(CB):
+            nc.scalar.mul(pe_scaled[b][:], pe_sb[b], 1.0 / math.sqrt(C))
+
+        for b in range(last):
+            g = gs[b]
+            if b == 0:
+                for cols_of_half, offs_of_half in ((first, offs_first), (second, offs_second)):
+                    nc.vector.tensor_tensor(
+                        g[:, cols_of_half],
+                        tables[b][:].indirect(offsets[:, offs_of_half]),
+                        pe_scaled[b][:, cols_of_half],
+                        ALU.add,
+                    )
+                nc.tensor.matmul(centre_ps[:], block_averager[:], g[:, first], start=True, stop=True)
+                nc.tensor.matmul(delta_ps[:], minus_two[:], g[:, first], start=True, stop=False)
+                nc.vector.tensor_tensor(pe_centred[:], pe_scaled[last][:, first], centre_ps[:], ALU.subtract)
+            else:
+                nc.vector.tensor_tensor(g[:], tables[b][:].indirect(offsets[:]), pe_scaled[b][:], ALU.add)
+                nc.tensor.matmul(delta_ps[:], averager[:], g[:, first], start=False, stop=False)
+            nc.tensor.matmul(mean_ps[:], averager[:], g[:, second], start=(b == 0), stop=False)
+            nc.vector.tensor_tensor(ds[b][:], g[:, first], centre_ps[:], ALU.subtract)
+            nc.scalar.activation(squares[b][:], ds[b][:], FUNC.Square)
+            nc.tensor.matmul(square_ps[:], averager[:], squares[b][:], start=(b == 0), stop=False)
+
+        nc.vector.tensor_tensor(ds[last][:], tables[last][:].indirect(offsets[:, offs_first]), pe_centred[:], ALU.add)
+        nc.tensor.matmul(delta_ps[:], averager[:], ds[last][:], start=False, stop=True)
+        nc.scalar.activation(squares[last][:], ds[last][:], FUNC.Square)
+        nc.tensor.matmul(square_ps[:], averager[:], squares[last][:], start=False, stop=True)
+        nc.vector.tensor_tensor(
+            gs[last][:, second], tables[last][:].indirect(offsets[:, offs_second]), pe_scaled[last][:, second], ALU.add
+        )
+        nc.tensor.matmul(mean_ps[:], averager[:], gs[last][:, second], start=False, stop=True)
+
+        centred = [held.tile([P, N], F32, name=f"centred{b}") for b in range(CB)]
+        delta = held.tile([P, H], F32, name="delta")
+        delta_sq = held.tile([P, H], F32, name="delta_sq")
+        var = held.tile([P, H], F32, name="var")
+        rstd = held.tile([P, N], F32, name="rstd")
+        nc.vector.tensor_copy(delta[:], delta_ps[:])
+        nc.vector.tensor_tensor(delta_sq[:], delta[:], delta[:], ALU.mult)
+        nc.vector.tensor_tensor(var[:], square_ps[:], delta_sq[:], ALU.subtract)
+        nc.scalar.activation(rstd[:, first], var[:], FUNC.Abs_reciprocal_sqrt, bias=eps_col[:])
+
+        cols_ps = stats.tile([P, P], F32, name="cols_ps", tag="centre_ps")
         nc.tensor.transpose(cols_ps[:], rows[:], identity[:])
         cols = held.tile([P, 2 * CB + VB], F32, name="cols")
         nc.vector.tensor_copy(cols[:], cols_ps[:, 0 : 2 * CB + VB])
 
-        pe_scaled = held.tile([P, CB, N], F32, name="pe_scaled")
-        mean_ps = stats.tile([P, N], F32, name="mean_ps")
-        gs = []
+        var_ps = stats.tile([P, H], F32, name="var_ps", tag="delta_ps")
         for b in range(CB):
-            nc.scalar.mul(pe_scaled[:, b, :], pe_sb[:, b, :], 1.0 / math.sqrt(C))
-            g = held.tile([P, N], F32, name=f"g{b}")
-            pieces = 2 if b == CB - 1 else 1
-            width = N // pieces
-            for piece in range(pieces):
-                cols_of_piece = slice(piece * width, (piece + 1) * width)
-                nc.vector.tensor_tensor(
-                    g[:, cols_of_piece],
-                    tables[b][:].indirect(offsets[:, piece * width // 16 : (piece + 1) * width // 16]),
-                    pe_scaled[:, b, cols_of_piece],
-                    ALU.add,
-                )
-                last = b == CB - 1 and piece == pieces - 1
-                nc.tensor.matmul(mean_ps[:, cols_of_piece], averager[:], g[:, cols_of_piece], start=(b == 0), stop=last)
-            gs.append(g)
+            sq = held.tile([P, H], F32, name=f"second_sq{b}")
+            nc.vector.tensor_tensor(centred[b][:, second], gs[b][:, second], mean_ps[:], ALU.subtract)
+            nc.scalar.activation(sq[:], centred[b][:, second], FUNC.Square)
+            nc.tensor.matmul(var_ps[:], averager[:], sq[:], start=(b == 0), stop=(b == last))
+        nc.scalar.activation(rstd[:, second], var_ps[:], FUNC.Abs_reciprocal_sqrt, bias=eps_col[:])
 
-        var_ps = stats.tile([P, N], F32, name="var_ps")
-        centred = []
-        squares = []
-        last_two = held.tile([P, N], F32, name="last_two")
         for b in range(CB):
-            d = held.tile([P, N], F32, name=f"d{b}")
-            sq = held.tile([P, N], F32, name=f"sq{b}")
-            centred.append(d)
-            squares.append(sq)
-            pieces = 2 if b == CB - 1 else 1
-            width = N // pieces
-            for piece in range(pieces):
-                cols_of_piece = slice(piece * width, (piece + 1) * width)
-                nc.vector.tensor_tensor(d[:, cols_of_piece], gs[b][:, cols_of_piece], mean_ps[:, cols_of_piece], ALU.subtract)
-                nc.scalar.activation(sq[:, cols_of_piece], d[:, cols_of_piece], FUNC.Square)
-                if b < CB - 2:
-                    nc.tensor.matmul(var_ps[:], averager[:], sq[:], start=(b == 0), stop=False)
-                if b == CB - 1:
-                    nc.vector.tensor_tensor(
-                        last_two[:, cols_of_piece], squares[b - 1][:, cols_of_piece], sq[:, cols_of_piece], ALU.add
-                    )
-                    nc.tensor.matmul(
-                        var_ps[:, cols_of_piece],
-                        averager[:],
-                        last_two[:, cols_of_piece],
-                        start=False,
-                        stop=(piece == pieces - 1),
-                    )
+            nc.vector.tensor_tensor(centred[b][:, first], ds[b][:], delta[:], ALU.subtract)
 
-        unread_ps = stats.tile([P, N], F32, name="unread_ps", tag="cols_ps")
-        for k in range(KEEP_BUSY):
-            nc.tensor.matmul(unread_ps[:], averager[:], last_two[:], start=True, stop=True)
+        normed = [held.tile([P, N], F32, name=f"normed{b}") for b in range(CB)]
+        ys = [held.tile([P, N], BF16, name=f"y{b}") for b in range(CB)]
 
-        rstd = held.tile([P, N], F32, name="rstd")
-        nc.scalar.activation(rstd[:], var_ps[:], FUNC.Abs_reciprocal_sqrt, bias=eps_col[:])
-
-        ys = []
-        for b in range(CB):
-            normed = held.tile([P, N], F32, name=f"normed{b}")
-            nc.vector.tensor_tensor(normed[:], centred[b][:], rstd[:], ALU.mult)
-            y = held.tile([P, N], BF16, name=f"y{b}")
-            gain_col, bias_col = cols[:, b : b + 1], cols[:, CB + b : CB + b + 1]
-            if b == 0:
-                nc.vector.tensor_scalar(y[:], normed[:], gain_col, bias_col, ALU.mult, ALU.add)
-            else:
-                nc.scalar.activation(y[:], normed[:], FUNC.Identity, bias=bias_col, scale=gain_col)
-            ys.append(y)
+        def make_y(tokens):
+            for b in range(CB):
+                nc.vector.tensor_tensor(normed[b][:, tokens], centred[b][:, tokens], rstd[:, tokens], ALU.mult)
+                gain_col, bias_col = cols[:, b : b + 1], cols[:, CB + b : CB + b + 1]
+                y, n = ys[b][:, tokens], normed[b][:, tokens]
+                if b == 0:
+                    nc.vector.tensor_scalar(y, n, gain_col, bias_col, ALU.mult, ALU.add)
+                else:
+                    nc.scalar.activation(y, n, FUNC.Identity, bias=bias_col, scale=gain_col)
 
         logit = held.tile([P, VB, N], F32, name="logit")
-        exits = 0
-        for v in range(VB):
-            pieces = 2 if v == VB - 1 else 1
-            width = N // pieces
-            for piece in range(pieces):
-                cols_of_piece = slice(piece * width, (piece + 1) * width)
-                logit_ps = logits.tile([P, width], F32, name="logit_ps")
+
+        def project(tokens):
+            for v in range(VB):
+                logit_ps = logits.tile([P, H], F32, name="logit_ps")
                 for b in range(CB):
-                    nc.tensor.matmul(
-                        logit_ps[:],
-                        wout_sb[:, b, v * P : (v + 1) * P],
-                        ys[b][:, cols_of_piece],
-                        start=(b == 0),
-                        stop=(b == CB - 1),
-                    )
+                    weights = wout_sb[:, b, v * P : (v + 1) * P]
+                    nc.tensor.matmul(logit_ps[:], weights, ys[b][:, tokens], start=(b == 0), stop=(b == last))
                 bout_col = cols[:, 2 * CB + v : 2 * CB + v + 1]
-                if exits % 2 == 0:
-                    nc.vector.tensor_scalar_add(logit[:, v, cols_of_piece], logit_ps[:], bout_col)
+                if v % 2 == 1:
+                    nc.vector.tensor_scalar_add(logit[:, v, tokens], logit_ps[:], bout_col)
+                    nc.sync.dma_start(out_pairs[:, v - 1 : v + 1, tokens], logit[:, v - 1 : v + 1, tokens])
                 else:
-                    nc.scalar.activation(logit[:, v, cols_of_piece], logit_ps[:], FUNC.Identity, bias=bout_col)
-                exits += 1
-                nc.sync.dma_start(out_blocks[v][:, cols_of_piece], logit[:, v, cols_of_piece])
+                    nc.scalar.activation(logit[:, v, tokens], logit_ps[:], FUNC.Identity, bias=bout_col)
+
+        make_y(first)
+        project(first)
+        make_y(second)
+        project(second)

@@ -29,24 +29,21 @@ def tile_decodertrans_kernel(tc, emb, pe, gain, bias, wout, bout, offs, out):
         tc.psum_pool(name="logits", bufs=4) as logits,
     ):
         offsets = held.tile([P, N // 16], U16, name="offsets")
-        tables = [held.tile([P, S], F32, name=f"table{b}") for b in range(CB)]
-        wout_sb = held.tile([P, CB, S], BF16, name="wout_sb")
-        pe_first = held.tile([P, N], F32, name="pe_first")
-        pe_rest = held.tile([P, CB - 1, N], F32, name="pe_rest")
-        pe_sb = [pe_first[:]] + [pe_rest[:, b, :] for b in range(CB - 1)]
-        pe_blocks = pe.rearrange("(b p) j -> p b j", p=P)
         nc.sync.dma_start(offsets[:], offs)
-        nc.scalar.dma_start(pe_first[:], pe_blocks[:, 0, :])
-        nc.sync.dma_start(tables[0][:], emb_blocks[0])
-        nc.sync.dma_start(pe_rest[:], pe_blocks[:, 1:CB, :])
-        for b in range(1, CB):
-            nc.sync.dma_start(tables[b][:], emb_blocks[b])
+        tables = []
+        for b in range(CB):
+            table = held.tile([P, S], F32, name=f"table{b}")
+            nc.sync.dma_start(table[:], emb_blocks[b])
+            tables.append(table)
         rows = held.tile([P, P], F32, name="rows")
         nc.gpsimd.memset(rows[:], 0.0)
         nc.sync.dma_start(rows[0:CB, :], gain.rearrange("(b p) o -> b (p o)", p=P))
         nc.sync.dma_start(rows[CB : 2 * CB, :], bias.rearrange("(b p) o -> b (p o)", p=P))
         nc.sync.dma_start(rows[2 * CB : 2 * CB + VB, :], bout.rearrange("(v p) o -> v (p o)", p=P))
+        wout_sb = held.tile([P, CB, S], BF16, name="wout_sb")
         nc.sync.dma_start(wout_sb[:], wout.rearrange("(b p) v -> p b v", p=P))
+        pe_sb = held.tile([P, CB, N], F32, name="pe_sb")
+        nc.scalar.dma_start(pe_sb[:], pe.rearrange("(b p) j -> p b j", p=P))
 
         averager = held.tile([P, P], F32, name="averager")
         nc.gpsimd.memset(averager[:], 1.0 / C)
@@ -73,7 +70,7 @@ def tile_decodertrans_kernel(tc, emb, pe, gain, bias, wout, bout, offs, out):
         square_ps = stats.tile([P, H], F32, name="square_ps")
         mean_ps = stats.tile([P, H], F32, name="mean_ps")
         for b in range(CB):
-            nc.scalar.mul(pe_scaled[b][:], pe_sb[b], 1.0 / math.sqrt(C))
+            nc.scalar.mul(pe_scaled[b][:], pe_sb[:, b, :], 1.0 / math.sqrt(C))
 
         for b in range(last):
             g = gs[b]
@@ -106,21 +103,19 @@ def tile_decodertrans_kernel(tc, emb, pe, gain, bias, wout, bout, offs, out):
         nc.tensor.matmul(mean_ps[:], averager[:], gs[last][:, second], start=False, stop=True)
 
         centred = [held.tile([P, N], F32, name=f"centred{b}") for b in range(CB)]
-        delta = held.tile([P, H], F32, name="delta")
         delta_sq = held.tile([P, H], F32, name="delta_sq")
         var = held.tile([P, H], F32, name="var")
         rstd = held.tile([P, N], F32, name="rstd")
-        nc.vector.tensor_copy(delta[:], delta_ps[:])
-        nc.vector.tensor_tensor(delta_sq[:], delta[:], delta[:], ALU.mult)
+        nc.scalar.activation(delta_sq[:], delta_ps[:], FUNC.Square)
         nc.vector.tensor_tensor(var[:], square_ps[:], delta_sq[:], ALU.subtract)
         nc.scalar.activation(rstd[:, first], var[:], FUNC.Abs_reciprocal_sqrt, bias=eps_col[:])
 
-        cols_ps = stats.tile([P, P], F32, name="cols_ps", tag="centre_ps")
+        cols_ps = stats.tile([P, P], F32, name="cols_ps", tag="square_ps")
         nc.tensor.transpose(cols_ps[:], rows[:], identity[:])
         cols = held.tile([P, 2 * CB + VB], F32, name="cols")
         nc.vector.tensor_copy(cols[:], cols_ps[:, 0 : 2 * CB + VB])
 
-        var_ps = stats.tile([P, H], F32, name="var_ps", tag="delta_ps")
+        var_ps = stats.tile([P, H], F32, name="var_ps", tag="centre_ps")
         for b in range(CB):
             sq = held.tile([P, H], F32, name=f"second_sq{b}")
             nc.vector.tensor_tensor(centred[b][:, second], gs[b][:, second], mean_ps[:], ALU.subtract)
@@ -129,7 +124,7 @@ def tile_decodertrans_kernel(tc, emb, pe, gain, bias, wout, bout, offs, out):
         nc.scalar.activation(rstd[:, second], var_ps[:], FUNC.Abs_reciprocal_sqrt, bias=eps_col[:])
 
         for b in range(CB):
-            nc.vector.tensor_tensor(centred[b][:, first], ds[b][:], delta[:], ALU.subtract)
+            nc.vector.tensor_tensor(centred[b][:, first], ds[b][:], delta_ps[:], ALU.subtract)
 
         normed = [held.tile([P, N], F32, name=f"normed{b}") for b in range(CB)]
         ys = [held.tile([P, N], BF16, name=f"y{b}") for b in range(CB)]
@@ -147,17 +142,22 @@ def tile_decodertrans_kernel(tc, emb, pe, gain, bias, wout, bout, offs, out):
         logit = held.tile([P, VB, N], F32, name="logit")
 
         def project(tokens):
-            for v in range(VB):
-                logit_ps = logits.tile([P, H], F32, name="logit_ps")
-                for b in range(CB):
-                    weights = wout_sb[:, b, v * P : (v + 1) * P]
-                    nc.tensor.matmul(logit_ps[:], weights, ys[b][:, tokens], start=(b == 0), stop=(b == last))
-                bout_col = cols[:, 2 * CB + v : 2 * CB + v + 1]
-                if v % 2 == 1:
-                    nc.vector.tensor_scalar_add(logit[:, v, tokens], logit_ps[:], bout_col)
-                    nc.sync.dma_start(out_pairs[:, v - 1 : v + 1, tokens], logit[:, v - 1 : v + 1, tokens])
-                else:
-                    nc.scalar.activation(logit[:, v, tokens], logit_ps[:], FUNC.Identity, bias=bout_col)
+            for pair in range(VB // 2):
+                logit_ps = logits.tile([P, 2, H], F32, name="logit_ps")
+                for k in range(2):
+                    v = 2 * pair + k
+                    for b in range(CB):
+                        weights = wout_sb[:, b, v * P : (v + 1) * P]
+                        nc.tensor.matmul(logit_ps[:, k, :], weights, ys[b][:, tokens], start=(b == 0), stop=(b == last))
+                for k in range(2):
+                    v = 2 * pair + k
+                    bout_col = cols[:, 2 * CB + v : 2 * CB + v + 1]
+                    if pair % 2 == 0:
+                        nc.scalar.activation(logit[:, v, tokens], logit_ps[:, k, :], FUNC.Identity, bias=bout_col)
+                    else:
+                        nc.vector.tensor_scalar_add(logit[:, v, tokens], logit_ps[:, k, :], bout_col)
+                rows_of_pair = slice(2 * pair, 2 * pair + 2)
+                nc.sync.dma_start(out_pairs[:, rows_of_pair, tokens], logit[:, rows_of_pair, tokens])
 
         make_y(first)
         project(first)

@@ -30,6 +30,9 @@ def tile_decodertrans_kernel(tc, emb, pe, gain, bias, wout, bout, offs, out):
     ):
         offsets = held.tile([P, N // 16], U16, name="offsets")
         nc.sync.dma_start(offsets[:], offs)
+        pe_blocks = pe.rearrange("(b p) j -> p b j", p=P)
+        pe_first = held.tile([P, N], F32, name="pe_first")
+        nc.scalar.dma_start(pe_first[:], pe_blocks[:, 0, :])
         tables = []
         for b in range(CB):
             table = held.tile([P, S], F32, name=f"table{b}")
@@ -42,8 +45,6 @@ def tile_decodertrans_kernel(tc, emb, pe, gain, bias, wout, bout, offs, out):
         nc.sync.dma_start(rows[2 * CB : 2 * CB + VB, :], bout.rearrange("(v p) o -> v (p o)", p=P))
         wout_sb = held.tile([P, CB, S], BF16, name="wout_sb")
         nc.sync.dma_start(wout_sb[:], wout.rearrange("(b p) v -> p b v", p=P))
-        pe_sb = held.tile([P, CB, N], F32, name="pe_sb")
-        nc.scalar.dma_start(pe_sb[:], pe.rearrange("(b p) j -> p b j", p=P))
 
         averager = held.tile([P, P], F32, name="averager")
         nc.gpsimd.memset(averager[:], 1.0 / C)
@@ -58,6 +59,9 @@ def tile_decodertrans_kernel(tc, emb, pe, gain, bias, wout, bout, offs, out):
 
         warmed = held.tile([P, 1], F32, name="warmed")
         nc.scalar.activation(warmed[:], eps_col[:], FUNC.Abs_reciprocal_sqrt)
+        pe_rest = held.tile([P, CB - 1, N], F32, name="pe_rest")
+        nc.scalar.dma_start(pe_rest[:], pe_blocks[:, 1:CB, :])
+        pe_sb = [pe_first[:]] + [pe_rest[:, b, :] for b in range(CB - 1)]
 
         last = CB - 1
         pe_scaled = [held.tile([P, N], F32, name=f"pe_scaled{b}") for b in range(CB)]
@@ -70,7 +74,7 @@ def tile_decodertrans_kernel(tc, emb, pe, gain, bias, wout, bout, offs, out):
         square_ps = stats.tile([P, H], F32, name="square_ps")
         mean_ps = stats.tile([P, H], F32, name="mean_ps")
         for b in range(CB):
-            nc.scalar.mul(pe_scaled[b][:], pe_sb[:, b, :], 1.0 / math.sqrt(C))
+            nc.scalar.mul(pe_scaled[b][:], pe_sb[b], 1.0 / math.sqrt(C))
 
         for b in range(last):
             g = gs[b]

@@ -50,8 +50,8 @@ def tile_decodertrans_kernel(tc, emb, pe, gain, bias, wout, bout, offs, out):
         nc.gpsimd.memset(averager[:], 1.0 / C)
         block_averager = held.tile([P, P], F32, name="block_averager")
         nc.gpsimd.memset(block_averager[:], 1.0 / P)
-        minus_two = held.tile([P, P], F32, name="minus_two")
-        nc.gpsimd.memset(minus_two[:], -2.0 / C)
+        minus_averager = held.tile([P, P], F32, name="minus_averager")
+        nc.gpsimd.memset(minus_averager[:], -1.0 / C)
         eps_col = held.tile([P, 1], F32, name="eps_col")
         nc.gpsimd.memset(eps_col[:], EPS / C)
         identity = held.tile([P, P], F32, name="identity")
@@ -65,46 +65,47 @@ def tile_decodertrans_kernel(tc, emb, pe, gain, bias, wout, bout, offs, out):
 
         last = CB - 1
         pe_scaled = [held.tile([P, N], F32, name=f"pe_scaled{b}") for b in range(CB)]
+        for b in range(CB):
+            nc.scalar.mul(pe_scaled[b][:], pe_sb[b], 1.0 / math.sqrt(C))
         gs = [held.tile([P, N], F32, name=f"g{b}") for b in range(CB)]
         ds = [held.tile([P, H], F32, name=f"d{b}") for b in range(CB)]
         squares = [held.tile([P, H], F32, name=f"sq{b}") for b in range(CB)]
         centre_ps = stats.tile([P, H], F32, name="centre_ps")
-        pe_centred = held.tile([P, H], F32, name="pe_centred")
         delta_ps = stats.tile([P, H], F32, name="delta_ps")
         square_ps = stats.tile([P, H], F32, name="square_ps")
         mean_ps = stats.tile([P, H], F32, name="mean_ps")
-        for b in range(CB):
-            nc.scalar.mul(pe_scaled[b][:], pe_sb[b], 1.0 / math.sqrt(C))
 
-        for b in range(last):
-            g = gs[b]
-            if b == 0:
-                for cols_of_half, offs_of_half in ((first, offs_first), (second, offs_second)):
-                    nc.vector.tensor_tensor(
-                        g[:, cols_of_half],
-                        tables[b][:].indirect(offsets[:, offs_of_half]),
-                        pe_scaled[b][:, cols_of_half],
-                        ALU.add,
-                    )
-                nc.tensor.matmul(centre_ps[:], block_averager[:], g[:, first], start=True, stop=True)
-                nc.tensor.matmul(delta_ps[:], minus_two[:], g[:, first], start=True, stop=False)
-                nc.vector.tensor_tensor(pe_centred[:], pe_scaled[last][:, first], centre_ps[:], ALU.subtract)
-            else:
-                nc.vector.tensor_tensor(g[:], tables[b][:].indirect(offsets[:]), pe_scaled[b][:], ALU.add)
-                nc.tensor.matmul(delta_ps[:], averager[:], g[:, first], start=False, stop=False)
-            nc.tensor.matmul(mean_ps[:], averager[:], g[:, second], start=(b == 0), stop=False)
-            nc.vector.tensor_tensor(ds[b][:], g[:, first], centre_ps[:], ALU.subtract)
+        def look_up(out, b, tokens, addend):
+            offsets_of_tokens = offsets[:, tokens.start // 16 : tokens.stop // 16]
+            nc.vector.tensor_tensor(out, tables[b][:].indirect(offsets_of_tokens), addend, ALU.add)
+
+        def add_squares(b):
             nc.scalar.activation(squares[b][:], ds[b][:], FUNC.Square)
-            nc.tensor.matmul(square_ps[:], averager[:], squares[b][:], start=(b == 0), stop=False)
+            nc.tensor.matmul(square_ps[:], averager[:], squares[b][:], start=(b == 0), stop=(b == last))
 
-        nc.vector.tensor_tensor(ds[last][:], tables[last][:].indirect(offsets[:, offs_first]), pe_centred[:], ALU.add)
-        nc.tensor.matmul(delta_ps[:], averager[:], ds[last][:], start=False, stop=True)
-        nc.scalar.activation(squares[last][:], ds[last][:], FUNC.Square)
-        nc.tensor.matmul(square_ps[:], averager[:], squares[last][:], start=False, stop=True)
-        nc.vector.tensor_tensor(
-            gs[last][:, second], tables[last][:].indirect(offsets[:, offs_second]), pe_scaled[last][:, second], ALU.add
-        )
-        nc.tensor.matmul(mean_ps[:], averager[:], gs[last][:, second], start=False, stop=True)
+        look_up(gs[0][:, first], 0, first, pe_scaled[0][:, first])
+        nc.tensor.matmul(centre_ps[:], block_averager[:], gs[0][:, first], start=True, stop=True)
+        nc.tensor.matmul(delta_ps[:], minus_averager[:], gs[0][:, first], start=True, stop=False)
+        look_up(gs[0][:, second], 0, second, pe_scaled[0][:, second])
+        nc.tensor.matmul(mean_ps[:], averager[:], gs[0][:, second], start=True, stop=False)
+        pe_centred = [held.tile([P, H], F32, name=f"pe_centred{b}") for b in range(2, CB)]
+        for b in range(2, CB):
+            nc.vector.tensor_tensor(pe_centred[b - 2][:], pe_scaled[b][:, first], centre_ps[:], ALU.subtract)
+        nc.vector.tensor_tensor(ds[0][:], gs[0][:, first], centre_ps[:], ALU.subtract)
+        add_squares(0)
+
+        look_up(gs[1][:], 1, slice(0, N), pe_scaled[1][:])
+        nc.vector.tensor_tensor(ds[1][:], gs[1][:, first], centre_ps[:], ALU.subtract)
+        nc.tensor.matmul(delta_ps[:], averager[:], gs[1][:, first], start=False, stop=False)
+        nc.tensor.matmul(mean_ps[:], averager[:], gs[1][:, second], start=False, stop=False)
+        add_squares(1)
+
+        for b in range(2, CB):
+            look_up(ds[b][:], b, first, pe_centred[b - 2][:])
+            nc.tensor.matmul(delta_ps[:], averager[:], ds[b][:], start=False, stop=(b == last))
+            add_squares(b)
+            look_up(gs[b][:, second], b, second, pe_scaled[b][:, second])
+            nc.tensor.matmul(mean_ps[:], averager[:], gs[b][:, second], start=False, stop=(b == last))
 
         centred = [held.tile([P, N], F32, name=f"centred{b}") for b in range(CB)]
         delta_sq = held.tile([P, H], F32, name="delta_sq")
@@ -114,12 +115,12 @@ def tile_decodertrans_kernel(tc, emb, pe, gain, bias, wout, bout, offs, out):
         nc.vector.tensor_tensor(var[:], square_ps[:], delta_sq[:], ALU.subtract)
         nc.scalar.activation(rstd[:, first], var[:], FUNC.Abs_reciprocal_sqrt, bias=eps_col[:])
 
-        cols_ps = stats.tile([P, P], F32, name="cols_ps", tag="square_ps")
+        cols_ps = stats.tile([P, P], F32, name="cols_ps", tag="centre_ps")
         nc.tensor.transpose(cols_ps[:], rows[:], identity[:])
         cols = held.tile([P, 2 * CB + VB], F32, name="cols")
         nc.vector.tensor_copy(cols[:], cols_ps[:, 0 : 2 * CB + VB])
 
-        var_ps = stats.tile([P, H], F32, name="var_ps", tag="centre_ps")
+        var_ps = stats.tile([P, H], F32, name="var_ps", tag="square_ps")
         for b in range(CB):
             sq = held.tile([P, H], F32, name=f"second_sq{b}")
             nc.vector.tensor_tensor(centred[b][:, second], gs[b][:, second], mean_ps[:], ALU.subtract)
@@ -146,20 +147,26 @@ def tile_decodertrans_kernel(tc, emb, pe, gain, bias, wout, bout, offs, out):
         logit = held.tile([P, VB, N], F32, name="logit")
 
         def project(tokens):
+            pairs = [logits.tile([P, 2, H], F32, name="logit_ps") for pair in range(VB // 2)]
+
+            def accumulate(pair, k, b):
+                v = 2 * pair + k
+                weights = wout_sb[:, b, v * P : (v + 1) * P]
+                nc.tensor.matmul(pairs[pair][:, k, :], weights, ys[b][:, tokens], start=(b == 0), stop=(b == last))
+
+            for b in range(CB):
+                for pair in range(VB // 2):
+                    accumulate(pair, 0, b)
             for pair in range(VB // 2):
-                logit_ps = logits.tile([P, 2, H], F32, name="logit_ps")
-                for k in range(2):
-                    v = 2 * pair + k
-                    for b in range(CB):
-                        weights = wout_sb[:, b, v * P : (v + 1) * P]
-                        nc.tensor.matmul(logit_ps[:, k, :], weights, ys[b][:, tokens], start=(b == 0), stop=(b == last))
+                for b in range(CB):
+                    accumulate(pair, 1, b)
                 for k in range(2):
                     v = 2 * pair + k
                     bout_col = cols[:, 2 * CB + v : 2 * CB + v + 1]
                     if pair % 2 == 0:
-                        nc.scalar.activation(logit[:, v, tokens], logit_ps[:, k, :], FUNC.Identity, bias=bout_col)
+                        nc.scalar.activation(logit[:, v, tokens], pairs[pair][:, k, :], FUNC.Identity, bias=bout_col)
                     else:
-                        nc.vector.tensor_scalar_add(logit[:, v, tokens], logit_ps[:, k, :], bout_col)
+                        nc.vector.tensor_scalar_add(logit[:, v, tokens], pairs[pair][:, k, :], bout_col)
                 rows_of_pair = slice(2 * pair, 2 * pair + 2)
                 nc.sync.dma_start(out_pairs[:, rows_of_pair, tokens], logit[:, rows_of_pair, tokens])
 

@@ -19,9 +19,8 @@ FUNC = mybir.ActivationFunctionType
 def tile_decodertrans_kernel(tc, emb, pe, gain, bias, wout, bout, offs, out):
     nc = tc.nc
     emb_blocks = emb.rearrange("(b p) s -> b p s", p=P)
-    out_pairs = out.rearrange("(v p) j -> p v j", p=P)
+    out_blocks = out.rearrange("(v p) j -> v p j", p=P)
     first, second = slice(0, H), slice(H, N)
-    offs_first, offs_second = slice(0, H // 16), slice(H // 16, N // 16)
 
     with (
         tc.tile_pool(name="held", bufs=1) as held,
@@ -146,31 +145,32 @@ def tile_decodertrans_kernel(tc, emb, pe, gain, bias, wout, bout, offs, out):
 
         logit = held.tile([P, VB, N], F32, name="logit")
 
-        def project(tokens):
-            pairs = [logits.tile([P, 2, H], F32, name="logit_ps") for pair in range(VB // 2)]
+        def accumulate(out_ps, v, b, tokens):
+            weights = wout_sb[:, b, v * P : (v + 1) * P]
+            nc.tensor.matmul(out_ps, weights, ys[b][:, tokens], start=(b == 0), stop=(b == last))
 
-            def accumulate(pair, k, b):
-                v = 2 * pair + k
-                weights = wout_sb[:, b, v * P : (v + 1) * P]
-                nc.tensor.matmul(pairs[pair][:, k, :], weights, ys[b][:, tokens], start=(b == 0), stop=(b == last))
-
-            for b in range(CB):
-                for pair in range(VB // 2):
-                    accumulate(pair, 0, b)
-            for pair in range(VB // 2):
-                for b in range(CB):
-                    accumulate(pair, 1, b)
-                for k in range(2):
-                    v = 2 * pair + k
-                    bout_col = cols[:, 2 * CB + v : 2 * CB + v + 1]
-                    if pair % 2 == 0:
-                        nc.scalar.activation(logit[:, v, tokens], pairs[pair][:, k, :], FUNC.Identity, bias=bout_col)
-                    else:
-                        nc.vector.tensor_scalar_add(logit[:, v, tokens], pairs[pair][:, k, :], bout_col)
-                rows_of_pair = slice(2 * pair, 2 * pair + 2)
-                nc.sync.dma_start(out_pairs[:, rows_of_pair, tokens], logit[:, rows_of_pair, tokens])
+        def leave_psum(out_ps, v, tokens, on_vector):
+            bout_col = cols[:, 2 * CB + v : 2 * CB + v + 1]
+            if on_vector:
+                nc.vector.tensor_scalar_add(logit[:, v, tokens], out_ps, bout_col)
+            else:
+                nc.scalar.activation(logit[:, v, tokens], out_ps, FUNC.Identity, bias=bout_col)
 
         make_y(first)
-        project(first)
+        pairs = [logits.tile([P, 2, H], F32, name="pair_ps", tag="logit_ps") for pair in range(VB // 2)]
+        for b in range(CB):
+            for pair in range(VB // 2):
+                accumulate(pairs[pair][:, 0, :], 2 * pair, b, first)
+        for pair in range(VB // 2):
+            for b in range(CB):
+                accumulate(pairs[pair][:, 1, :], 2 * pair + 1, b, first)
+            for k in range(2):
+                leave_psum(pairs[pair][:, k, :], 2 * pair + k, first, on_vector=(pair % 2 == 1))
+
         make_y(second)
-        project(second)
+        for v in range(VB):
+            logit_ps = logits.tile([P, H], F32, name="logit_ps")
+            for b in range(CB):
+                accumulate(logit_ps[:], v, b, second)
+            leave_psum(logit_ps[:], v, second, on_vector=(v % 2 == 1))
+            nc.sync.dma_start(out_blocks[v], logit[:, v, :])

@@ -32,16 +32,14 @@ def tile_decodertrans_kernel(tc, emb, pe, gain, bias, wout, bout, offs, out):
         pe_blocks = pe.rearrange("(b p) j -> p b j", p=P)
         pe_first = held.tile([P, N], F32, name="pe_first")
         nc.scalar.dma_start(pe_first[:], pe_blocks[:, 0, :])
+        pe_rest = held.tile([P, CB - 1, N], F32, name="pe_rest")
+        nc.scalar.dma_start(pe_rest[:], pe_blocks[:, 1:CB, :])
+        pe_sb = [pe_first[:]] + [pe_rest[:, b, :] for b in range(CB - 1)]
         tables = []
         for b in range(CB):
             table = held.tile([P, S], F32, name=f"table{b}")
             nc.sync.dma_start(table[:], emb_blocks[b])
             tables.append(table)
-        rows = held.tile([P, P], F32, name="rows")
-        nc.gpsimd.memset(rows[:], 0.0)
-        nc.sync.dma_start(rows[0:CB, :], gain.rearrange("(b p) o -> b (p o)", p=P))
-        nc.sync.dma_start(rows[CB : 2 * CB, :], bias.rearrange("(b p) o -> b (p o)", p=P))
-        nc.sync.dma_start(rows[2 * CB : 2 * CB + VB, :], bout.rearrange("(v p) o -> v (p o)", p=P))
         wout_sb = held.tile([P, CB, S], BF16, name="wout_sb")
         nc.sync.dma_start(wout_sb[:], wout.rearrange("(b p) v -> p b v", p=P))
 
@@ -58,14 +56,17 @@ def tile_decodertrans_kernel(tc, emb, pe, gain, bias, wout, bout, offs, out):
 
         warmed = held.tile([P, 1], F32, name="warmed")
         nc.scalar.activation(warmed[:], eps_col[:], FUNC.Abs_reciprocal_sqrt)
-        pe_rest = held.tile([P, CB - 1, N], F32, name="pe_rest")
-        nc.scalar.dma_start(pe_rest[:], pe_blocks[:, 1:CB, :])
-        pe_sb = [pe_first[:]] + [pe_rest[:, b, :] for b in range(CB - 1)]
 
         last = CB - 1
         pe_scaled = [held.tile([P, N], F32, name=f"pe_scaled{b}") for b in range(CB)]
         for b in range(CB):
             nc.scalar.mul(pe_scaled[b][:], pe_sb[b], 1.0 / math.sqrt(C))
+        rows = held.tile([P, P], F32, name="rows")
+        nc.gpsimd.memset(rows[:], 0.0)
+        nc.scalar.dma_start(rows[0:CB, :], gain.rearrange("(b p) o -> b (p o)", p=P))
+        nc.scalar.dma_start(rows[CB : 2 * CB, :], bias.rearrange("(b p) o -> b (p o)", p=P))
+        nc.scalar.dma_start(rows[2 * CB : 2 * CB + VB, :], bout.rearrange("(v p) o -> v (p o)", p=P))
+
         gs = [held.tile([P, N], F32, name=f"g{b}") for b in range(CB)]
         ds = [held.tile([P, H], F32, name=f"d{b}") for b in range(CB)]
         squares = [held.tile([P, H], F32, name=f"sq{b}") for b in range(CB)]

@@ -35,6 +35,11 @@ def tile_decodertrans_kernel(tc, emb, pe, gain, bias, wout, bout, offs, out):
         pe_rest = held.tile([P, CB - 1, N], F32, name="pe_rest")
         nc.scalar.dma_start(pe_rest[:], pe_blocks[:, 1:CB, :])
         pe_sb = [pe_first[:]] + [pe_rest[:, b, :] for b in range(CB - 1)]
+        rows = held.tile([P, P], F32, name="rows")
+        nc.gpsimd.memset(rows[:], 0.0)
+        nc.scalar.dma_start(rows[0:CB, :], gain.rearrange("(b p) o -> b (p o)", p=P))
+        nc.scalar.dma_start(rows[CB : 2 * CB, :], bias.rearrange("(b p) o -> b (p o)", p=P))
+        nc.scalar.dma_start(rows[2 * CB : 2 * CB + VB, :], bout.rearrange("(v p) o -> v (p o)", p=P))
         tables = []
         for b in range(CB):
             table = held.tile([P, S], F32, name=f"table{b}")
@@ -45,10 +50,6 @@ def tile_decodertrans_kernel(tc, emb, pe, gain, bias, wout, bout, offs, out):
 
         averager = held.tile([P, P], F32, name="averager")
         nc.gpsimd.memset(averager[:], 1.0 / C)
-        block_averager = held.tile([P, P], F32, name="block_averager")
-        nc.gpsimd.memset(block_averager[:], 1.0 / P)
-        minus_averager = held.tile([P, P], F32, name="minus_averager")
-        nc.gpsimd.memset(minus_averager[:], -1.0 / C)
         eps_col = held.tile([P, 1], F32, name="eps_col")
         nc.gpsimd.memset(eps_col[:], EPS / C)
         identity = held.tile([P, P], F32, name="identity")
@@ -57,79 +58,48 @@ def tile_decodertrans_kernel(tc, emb, pe, gain, bias, wout, bout, offs, out):
         warmed = held.tile([P, 1], F32, name="warmed")
         nc.scalar.activation(warmed[:], eps_col[:], FUNC.Abs_reciprocal_sqrt)
 
-        last = CB - 1
-        pe_scaled = [held.tile([P, N], F32, name=f"pe_scaled{b}") for b in range(CB)]
-        for b in range(CB):
-            nc.scalar.mul(pe_scaled[b][:], pe_sb[b], 1.0 / math.sqrt(C))
-        rows = held.tile([P, P], F32, name="rows")
-        nc.gpsimd.memset(rows[:], 0.0)
-        nc.scalar.dma_start(rows[0:CB, :], gain.rearrange("(b p) o -> b (p o)", p=P))
-        nc.scalar.dma_start(rows[CB : 2 * CB, :], bias.rearrange("(b p) o -> b (p o)", p=P))
-        nc.scalar.dma_start(rows[2 * CB : 2 * CB + VB, :], bout.rearrange("(v p) o -> v (p o)", p=P))
-
-        gs = [held.tile([P, N], F32, name=f"g{b}") for b in range(CB)]
-        ds = [held.tile([P, H], F32, name=f"d{b}") for b in range(CB)]
-        squares = [held.tile([P, H], F32, name=f"sq{b}") for b in range(CB)]
-        centre_ps = stats.tile([P, H], F32, name="centre_ps")
-        delta_ps = stats.tile([P, H], F32, name="delta_ps")
-        square_ps = stats.tile([P, H], F32, name="square_ps")
-        mean_ps = stats.tile([P, H], F32, name="mean_ps")
-
-        def look_up(out, b, tokens, addend):
-            offsets_of_tokens = offsets[:, tokens.start // 16 : tokens.stop // 16]
-            nc.vector.tensor_tensor(out, tables[b][:].indirect(offsets_of_tokens), addend, ALU.add)
-
-        def add_squares(b):
-            nc.scalar.activation(squares[b][:], ds[b][:], FUNC.Square)
-            nc.tensor.matmul(square_ps[:], averager[:], squares[b][:], start=(b == 0), stop=(b == last))
-
-        look_up(gs[0][:, first], 0, first, pe_scaled[0][:, first])
-        nc.tensor.matmul(centre_ps[:], block_averager[:], gs[0][:, first], start=True, stop=True)
-        nc.tensor.matmul(delta_ps[:], minus_averager[:], gs[0][:, first], start=True, stop=False)
-        look_up(gs[0][:, second], 0, second, pe_scaled[0][:, second])
-        nc.tensor.matmul(mean_ps[:], averager[:], gs[0][:, second], start=True, stop=False)
-        pe_centred = [held.tile([P, H], F32, name=f"pe_centred{b}") for b in range(2, CB)]
-        for b in range(2, CB):
-            nc.vector.tensor_tensor(pe_centred[b - 2][:], pe_scaled[b][:, first], centre_ps[:], ALU.subtract)
-        nc.vector.tensor_tensor(ds[0][:], gs[0][:, first], centre_ps[:], ALU.subtract)
-        add_squares(0)
-
-        look_up(gs[1][:], 1, slice(0, N), pe_scaled[1][:])
-        nc.vector.tensor_tensor(ds[1][:], gs[1][:, first], centre_ps[:], ALU.subtract)
-        nc.tensor.matmul(delta_ps[:], averager[:], gs[1][:, first], start=False, stop=False)
-        nc.tensor.matmul(mean_ps[:], averager[:], gs[1][:, second], start=False, stop=False)
-        add_squares(1)
-
-        for b in range(2, CB):
-            look_up(ds[b][:], b, first, pe_centred[b - 2][:])
-            nc.tensor.matmul(delta_ps[:], averager[:], ds[b][:], start=False, stop=(b == last))
-            add_squares(b)
-            look_up(gs[b][:, second], b, second, pe_scaled[b][:, second])
-            nc.tensor.matmul(mean_ps[:], averager[:], gs[b][:, second], start=False, stop=(b == last))
-
-        centred = [held.tile([P, N], F32, name=f"centred{b}") for b in range(CB)]
-        delta_sq = held.tile([P, H], F32, name="delta_sq")
-        var = held.tile([P, H], F32, name="var")
-        rstd = held.tile([P, N], F32, name="rstd")
-        nc.scalar.activation(delta_sq[:], delta_ps[:], FUNC.Square)
-        nc.vector.tensor_tensor(var[:], square_ps[:], delta_sq[:], ALU.subtract)
-        nc.scalar.activation(rstd[:, first], var[:], FUNC.Abs_reciprocal_sqrt, bias=eps_col[:])
-
-        cols_ps = stats.tile([P, P], F32, name="cols_ps", tag="centre_ps")
+        cols_ps = stats.tile([P, P], F32, name="cols_ps")
         nc.tensor.transpose(cols_ps[:], rows[:], identity[:])
         cols = held.tile([P, 2 * CB + VB], F32, name="cols")
         nc.vector.tensor_copy(cols[:], cols_ps[:, 0 : 2 * CB + VB])
 
-        var_ps = stats.tile([P, H], F32, name="var_ps", tag="square_ps")
+        pe_scaled = [held.tile([P, N], F32, name=f"pe_scaled{b}") for b in range(CB)]
         for b in range(CB):
-            sq = held.tile([P, H], F32, name=f"second_sq{b}")
-            nc.vector.tensor_tensor(centred[b][:, second], gs[b][:, second], mean_ps[:], ALU.subtract)
-            nc.scalar.activation(sq[:], centred[b][:, second], FUNC.Square)
-            nc.tensor.matmul(var_ps[:], averager[:], sq[:], start=(b == 0), stop=(b == last))
-        nc.scalar.activation(rstd[:, second], var_ps[:], FUNC.Abs_reciprocal_sqrt, bias=eps_col[:])
+            nc.scalar.mul(pe_scaled[b][:], pe_sb[b], 1.0 / math.sqrt(C))
 
+        halves = [first, second]
+        last = CB - 1
+        gs = [held.tile([P, N], F32, name=f"g{b}") for b in range(CB)]
+        mean_ps = stats.tile([P, N], F32, name="mean_ps")
         for b in range(CB):
-            nc.vector.tensor_tensor(centred[b][:, first], ds[b][:], delta_ps[:], ALU.subtract)
+            for piece in halves if b == last else [slice(0, N)]:
+                offsets_of_piece = offsets[:, piece.start // 16 : piece.stop // 16]
+                nc.vector.tensor_tensor(
+                    gs[b][:, piece], tables[b][:].indirect(offsets_of_piece), pe_scaled[b][:, piece], ALU.add
+                )
+                closing = b == last and piece == second
+                nc.tensor.matmul(mean_ps[:, piece], averager[:], gs[b][:, piece], start=(b == 0), stop=closing)
+
+        centred = [held.tile([P, N], F32, name=f"d{b}") for b in range(CB)]
+        squares = [held.tile([P, N], F32, name=f"sq{b}") for b in range(CB)]
+        two_squares = [held.tile([P, H], F32, name=f"two_squares{k}") for k in range(CB // 2)]
+        rstd = held.tile([P, N], F32, name="rstd")
+        var_ps = [stats.tile([P, H], F32, name=f"var_ps{h}") for h in range(2)]
+        for h, tokens in enumerate(halves):
+            for b in range(CB):
+                nc.vector.tensor_tensor(centred[b][:, tokens], gs[b][:, tokens], mean_ps[:, tokens], ALU.subtract)
+                nc.scalar.activation(squares[b][:, tokens], centred[b][:, tokens], FUNC.Square)
+            if h == 0:
+                summands = [squares[b][:, tokens] for b in range(CB)]
+            else:
+                for k in range(CB // 2):
+                    nc.vector.tensor_tensor(
+                        two_squares[k][:], squares[2 * k][:, tokens], squares[2 * k + 1][:, tokens], ALU.add
+                    )
+                summands = [two_squares[k][:] for k in range(CB // 2)]
+            for k, summand in enumerate(summands):
+                nc.tensor.matmul(var_ps[h][:], averager[:], summand, start=(k == 0), stop=(k == len(summands) - 1))
+            nc.scalar.activation(rstd[:, tokens], var_ps[h][:], FUNC.Abs_reciprocal_sqrt, bias=eps_col[:])
 
         normed = [held.tile([P, N], F32, name=f"normed{b}") for b in range(CB)]
         ys = [held.tile([P, N], BF16, name=f"y{b}") for b in range(CB)]

@@ -29,17 +29,6 @@ def tile_decodertrans_kernel(tc, emb, pe, gain, bias, wout, bout, offs, out):
     ):
         offsets = held.tile([P, N // 16], U16, name="offsets")
         nc.sync.dma_start(offsets[:], offs)
-        pe_blocks = pe.rearrange("(b p) j -> p b j", p=P)
-        pe_first = held.tile([P, N], F32, name="pe_first")
-        nc.scalar.dma_start(pe_first[:], pe_blocks[:, 0, :])
-        pe_rest = held.tile([P, CB - 1, N], F32, name="pe_rest")
-        nc.scalar.dma_start(pe_rest[:], pe_blocks[:, 1:CB, :])
-        pe_sb = [pe_first[:]] + [pe_rest[:, b, :] for b in range(CB - 1)]
-        rows = held.tile([P, P], F32, name="rows")
-        nc.gpsimd.memset(rows[:], 0.0)
-        nc.scalar.dma_start(rows[0:CB, :], gain.rearrange("(b p) o -> b (p o)", p=P))
-        nc.scalar.dma_start(rows[CB : 2 * CB, :], bias.rearrange("(b p) o -> b (p o)", p=P))
-        nc.scalar.dma_start(rows[2 * CB : 2 * CB + VB, :], bout.rearrange("(v p) o -> v (p o)", p=P))
         tables = []
         for b in range(CB):
             table = held.tile([P, S], F32, name=f"table{b}")
@@ -47,6 +36,13 @@ def tile_decodertrans_kernel(tc, emb, pe, gain, bias, wout, bout, offs, out):
             tables.append(table)
         wout_sb = held.tile([P, CB, S], BF16, name="wout_sb")
         nc.sync.dma_start(wout_sb[:], wout.rearrange("(b p) v -> p b v", p=P))
+        pe_sb = held.tile([P, CB, N], F32, name="pe_sb")
+        nc.scalar.dma_start(pe_sb[:], pe.rearrange("(b p) j -> p b j", p=P))
+        rows = held.tile([P, P], F32, name="rows")
+        nc.gpsimd.memset(rows[:], 0.0)
+        nc.scalar.dma_start(rows[0:CB, :], gain.rearrange("(b p) o -> b (p o)", p=P))
+        nc.scalar.dma_start(rows[CB : 2 * CB, :], bias.rearrange("(b p) o -> b (p o)", p=P))
+        nc.scalar.dma_start(rows[2 * CB : 2 * CB + VB, :], bout.rearrange("(v p) o -> v (p o)", p=P))
 
         averager = held.tile([P, P], F32, name="averager")
         nc.gpsimd.memset(averager[:], 1.0 / C)
@@ -65,7 +61,7 @@ def tile_decodertrans_kernel(tc, emb, pe, gain, bias, wout, bout, offs, out):
 
         pe_scaled = [held.tile([P, N], F32, name=f"pe_scaled{b}") for b in range(CB)]
         for b in range(CB):
-            nc.scalar.mul(pe_scaled[b][:], pe_sb[b], 1.0 / math.sqrt(C))
+            nc.scalar.mul(pe_scaled[b][:], pe_sb[:, b, :], 1.0 / math.sqrt(C))
 
         halves = [first, second]
         last = CB - 1

import math

import concourse.mybir as mybir
from concourse.masks import make_identity

P = 128
C, S, N = 512, 1024, 256
CB = C // P
VB = S // P
EPS = 1e-5
FLOPS = 2 * C * S * N
H = N // 2

F32, BF16, U16 = mybir.dt.float32, mybir.dt.bfloat16, mybir.dt.uint16
ALU = mybir.AluOpType
FUNC = mybir.ActivationFunctionType


def tile_decodertrans_kernel(tc, emb, pe, gain, bias, wout, bout, offs, out):
    nc = tc.nc
    emb_blocks = emb.rearrange("(b p) s -> b p s", p=P)
    out_blocks = out.rearrange("(v p) j -> v p j", p=P)
    first, second = slice(0, H), slice(H, N)

    with (
        tc.tile_pool(name="held", bufs=1) as held,
        tc.psum_pool(name="stats", bufs=1) as stats,
        tc.psum_pool(name="logits", bufs=4) as logits,
    ):
        offsets = held.tile([P, N // 16], U16, name="offsets")
        nc.sync.dma_start(offsets[:], offs)
        tables = []
        for b in range(CB):
            table = held.tile([P, S], F32, name=f"table{b}")
            nc.sync.dma_start(table[:], emb_blocks[b])
            tables.append(table)
        wout_sb = held.tile([P, CB, S], BF16, name="wout_sb")
        nc.sync.dma_start(wout_sb[:], wout.rearrange("(b p) v -> p b v", p=P))
        pe_sb = held.tile([P, CB, N], F32, name="pe_sb")
        nc.scalar.dma_start(pe_sb[:], pe.rearrange("(b p) j -> p b j", p=P))
        rows = held.tile([P, P], F32, name="rows")
        nc.gpsimd.memset(rows[:], 0.0)
        nc.scalar.dma_start(rows[0:CB, :], gain.rearrange("(b p) o -> b (p o)", p=P))
        nc.scalar.dma_start(rows[CB : 2 * CB, :], bias.rearrange("(b p) o -> b (p o)", p=P))
        nc.scalar.dma_start(rows[2 * CB : 2 * CB + VB, :], bout.rearrange("(v p) o -> v (p o)", p=P))

        averager = held.tile([P, P], F32, name="averager")
        nc.gpsimd.memset(averager[:], 1.0 / C)
        eps_col = held.tile([P, 1], F32, name="eps_col")
        nc.gpsimd.memset(eps_col[:], EPS / C)
        identity = held.tile([P, P], F32, name="identity")
        make_identity(nc, identity[:])

        warmed = held.tile([P, 1], F32, name="warmed")
        nc.scalar.activation(warmed[:], eps_col[:], FUNC.Abs_reciprocal_sqrt)

        cols_ps = stats.tile([P, P], F32, name="cols_ps")
        nc.tensor.transpose(cols_ps[:], rows[:], identity[:])
        cols = held.tile([P, 2 * CB + VB], F32, name="cols")
        nc.vector.tensor_copy(cols[:], cols_ps[:, 0 : 2 * CB + VB])

        pe_scaled = [held.tile([P, N], F32, name=f"pe_scaled{b}") for b in range(CB)]
        for b in range(CB):
            nc.scalar.mul(pe_scaled[b][:], pe_sb[:, b, :], 1.0 / math.sqrt(C))

        halves = [first, second]
        last = CB - 1
        gs = [held.tile([P, N], F32, name=f"g{b}") for b in range(CB)]
        mean_ps = stats.tile([P, N], F32, name="mean_ps")
        for b in range(CB):
            for piece in halves if b == last else [slice(0, N)]:
                offsets_of_piece = offsets[:, piece.start // 16 : piece.stop // 16]
                nc.vector.tensor_tensor(
                    gs[b][:, piece], tables[b][:].indirect(offsets_of_piece), pe_scaled[b][:, piece], ALU.add
                )
                closing = b == last and piece == second
                nc.tensor.matmul(mean_ps[:, piece], averager[:], gs[b][:, piece], start=(b == 0), stop=closing)

        centred = [held.tile([P, N], F32, name=f"d{b}") for b in range(CB)]
        squares = [held.tile([P, N], F32, name=f"sq{b}") for b in range(CB)]
        two_squares = [held.tile([P, H], F32, name=f"two_squares{k}") for k in range(CB // 2)]
        rstd = held.tile([P, N], F32, name="rstd")
        var_ps = [stats.tile([P, H], F32, name=f"var_ps{h}") for h in range(2)]
        for h, tokens in enumerate(halves):
            for b in range(CB):
                nc.vector.tensor_tensor(centred[b][:, tokens], gs[b][:, tokens], mean_ps[:, tokens], ALU.subtract)
                nc.scalar.activation(squares[b][:, tokens], centred[b][:, tokens], FUNC.Square)
            if h == 0:
                summands = [squares[b][:, tokens] for b in range(CB)]
            else:
                for k in range(CB // 2):
                    nc.vector.tensor_tensor(
                        two_squares[k][:], squares[2 * k][:, tokens], squares[2 * k + 1][:, tokens], ALU.add
                    )
                summands = [two_squares[k][:] for k in range(CB // 2)]
            for k, summand in enumerate(summands):
                nc.tensor.matmul(var_ps[h][:], averager[:], summand, start=(k == 0), stop=(k == len(summands) - 1))
            nc.scalar.activation(rstd[:, tokens], var_ps[h][:], FUNC.Abs_reciprocal_sqrt, bias=eps_col[:])

        normed = [held.tile([P, N], F32, name=f"normed{b}") for b in range(CB)]
        ys = [held.tile([P, N], BF16, name=f"y{b}") for b in range(CB)]

        def make_y(tokens):
            for b in range(CB):
                nc.vector.tensor_tensor(normed[b][:, tokens], centred[b][:, tokens], rstd[:, tokens], ALU.mult)
                gain_col, bias_col = cols[:, b : b + 1], cols[:, CB + b : CB + b + 1]
                y, n = ys[b][:, tokens], normed[b][:, tokens]
                if b == 0:
                    nc.vector.tensor_scalar(y, n, gain_col, bias_col, ALU.mult, ALU.add)
                else:
                    nc.scalar.activation(y, n, FUNC.Identity, bias=bias_col, scale=gain_col)

        logit = held.tile([P, VB, N], F32, name="logit")

        def accumulate(out_ps, v, b, tokens):
            weights = wout_sb[:, b, v * P : (v + 1) * P]
            nc.tensor.matmul(out_ps, weights, ys[b][:, tokens], start=(b == 0), stop=(b == last))

        def leave_psum(out_ps, v, tokens, on_vector):
            bout_col = cols[:, 2 * CB + v : 2 * CB + v + 1]
            if on_vector:
                nc.vector.tensor_scalar_add(logit[:, v, tokens], out_ps, bout_col)
            else:
                nc.scalar.activation(logit[:, v, tokens], out_ps, FUNC.Identity, bias=bout_col)

        make_y(first)
        pairs = [logits.tile([P, 2, H], F32, name="pair_ps", tag="logit_ps") for pair in range(VB // 2)]
        for b in range(CB):
            for pair in range(VB // 2):
                accumulate(pairs[pair][:, 0, :], 2 * pair, b, first)
        for pair in range(VB // 2):
            for b in range(CB):
                accumulate(pairs[pair][:, 1, :], 2 * pair + 1, b, first)
            for k in range(2):
                leave_psum(pairs[pair][:, k, :], 2 * pair + k, first, on_vector=(pair % 2 == 1))

        make_y(second)
        for v in range(VB):
            logit_ps = logits.tile([P, H], F32, name="logit_ps")
            for b in range(CB):
                accumulate(logit_ps[:], v, b, second)
            leave_psum(logit_ps[:], v, second, on_vector=(v % 2 == 1))
            nc.sync.dma_start(out_blocks[v], logit[:, v, :])
